import numpy as np
import ml_dtypes


def mxq(x, axis, fmt="e4m3"):
    dtype, down = {"e4m3": (ml_dtypes.float8_e4m3fn, 7), "e5m2": (ml_dtypes.float8_e5m2, 14)}[fmt]
    v = np.moveaxis(np.asarray(x, np.float32).astype(ml_dtypes.bfloat16).astype(np.float64), axis, -1)
    blocks = v.reshape(v.shape[:-1] + (-1, 32))
    amax = np.abs(blocks).max(-1, keepdims=True)
    byte = np.maximum(np.where(amax > 0, np.frexp(amax)[1] - 1 + 127, 0) - down, 1)
    scale = np.exp2(byte - 127.0)
    codes = (blocks / scale).astype(np.float32).astype(dtype).astype(np.float64)
    return np.moveaxis((codes * scale).reshape(v.shape), -1, axis)


WIDE = False


def mx_kscale(k):
    if not WIDE:
        return np.ones(k)
    levels = np.array([10, -10, 5, -5, 0])
    a = np.random.permutation(np.resize(levels, k // 512 * 4)).reshape(k // 512, 4)
    idx = np.arange(k)
    return np.exp2(a[idx // 512, idx % 128 // 32])


BF16 = ml_dtypes.bfloat16


def bf(x):
    return np.asarray(x, np.float32).astype(BF16)


def f64(x):
    return np.asarray(x).astype(np.float64)


E2M1 = np.array([0.0, 0.5, 1.0, 1.5, 2.0, 3.0, 4.0, 6.0, -0.0, -0.5, -1.0, -1.5, -2.0, -3.0, -4.0, -6.0])


def pack_weight(w, fmt):
    k, n = w.shape
    w = f64(bf(w)).reshape(k // 32, 32, n)
    amax = np.abs(w).max(1)
    if fmt == "e4m3":
        byte = np.frexp(amax)[1] - 1 + 127 - 7
    else:
        mant, ex = np.frexp(amax / 6.0)
        byte = np.where(mant > 0.5, ex, ex - 1) + 127
    byte = np.clip(np.where(amax > 0, byte, 1), 1, 254)
    scaled = (w * np.exp2(127.0 - byte)[:, None, :]).reshape(k, n).astype(np.float32)
    by_word = np.ascontiguousarray(scaled.reshape(k // 512, 128, 4, n).transpose(0, 1, 3, 2))
    if fmt == "e4m3":
        words = by_word.astype(ml_dtypes.float8_e4m3fn).view(np.uint8)
    else:
        c = by_word.astype(ml_dtypes.float4_e2m1fn).view(np.uint8) & 0xF
        words = c[..., 0::2] | (c[..., 1::2] << 4)
    return np.ascontiguousarray(words), np.ascontiguousarray(byte.astype(np.uint8).reshape(k // 512, 16, n))


def unpack_weight(words, scales, fmt):
    g, p, n, _ = words.shape
    if fmt == "e4m3":
        vals = np.ascontiguousarray(words).view(ml_dtypes.float8_e4m3fn).astype(np.float64)
    else:
        nib = np.empty((g, p, n, 4), np.uint8)
        nib[..., 0::2] = words & 0xF
        nib[..., 1::2] = words >> 4
        vals = E2M1[nib]
    vals = vals * np.repeat(np.exp2(scales.astype(np.float64) - 127.0), 8, axis=1)[..., None]
    return vals.transpose(0, 1, 3, 2).reshape(g * 512, n)


B, N, D, HID, HEADS = 4, 128, 3, 512, 128


def silu(v):
    e = np.exp(-np.abs(v))
    return v * np.where(v >= 0, 1.0, e) / (1.0 + e)


def pairwise_dist(c):
    diff = c[:, :, None, :] - c[:, None, :, :]
    sq = np.sum(diff * diff, axis=-1)
    safe = np.where(sq > 0, sq, 1.0)
    return np.where(sq > 0, np.sqrt(safe), 0.0)


def setup_inputs():
    t = np.maximum(mx_kscale(HID), 1.0) ** 2
    coords = bf(np.random.standard_normal((B, N, D)))
    w1 = bf(np.random.uniform(-1.0, 1.0, (1, HID)) * t[None, :])
    b1 = bf(np.random.uniform(-1.0, 1.0, HID) * t)
    w2_words, w2_scales = pack_weight(np.random.standard_normal((HID, HEADS)) / np.sqrt(HID) / t[:, None], "e4m3")
    b2 = bf(np.random.standard_normal(HEADS) * 0.3)
    return {"coords": coords,
            "w1": w1,
            "b1": b1,
            "w2_words": w2_words,
            "w2_scales": w2_scales,
            "b2": b2}


def reference(coords, w1, b1, w2_words, w2_scales, b2):
    d = pairwise_dist(f64(coords))
    h = silu(d[..., None] * f64(w1)[0] + f64(b1))
    b = (mxq(h, 3, "e4m3") @ unpack_weight(w2_words, w2_scales, "e4m3")) + f64(b2)
    return np.transpose(b, (0, 3, 1, 2))

@@ -1,0 +1,234 @@
+from contextlib import ExitStack
+
+import concourse.mybir as mybir
+from concourse.masks import make_identity
+
+F32 = mybir.dt.float32
+BF16 = mybir.dt.bfloat16
+I32 = mybir.dt.int32
+U32 = mybir.dt.uint32
+U8 = mybir.dt.uint8
+FP8X4 = mybir.dt.float8_e4m3fn_x4
+ACT = mybir.ActivationFunctionType
+ALU = mybir.AluOpType
+
+P = 128
+BATCH = 4
+POINTS = 128
+HALF = POINTS // 2
+DIMS = 3
+HIDDEN = 512
+HEADS = 128
+PACK = 4
+ROWS = 4
+STEP_PAIRS = ROWS * POINTS
+GROUPS = HALF // ROWS
+STEPS = BATCH * GROUPS
+BLOCK_PITCH = ROWS * POINTS + ROWS
+N_BLOCKS = POINTS // ROWS
+STORE_ROWS = 16
+STORE_GROUPS = STORE_ROWS // ROWS
+SCALAR_COLS = 48
+
+FLOPS = 2 * BATCH * POINTS * POINTS * HIDDEN * HEADS
+
+
+def tile_distancerelativebias_kernel(tc, coords, w1, b1, w2_words, w2_scales, b2, out):
+    nc = tc.nc
+    with ExitStack() as ctx:
+        const = ctx.enter_context(tc.tile_pool(name="const", bufs=1))
+        setup = ctx.enter_context(tc.tile_pool(name="setup", bufs=1))
+        hidden_pool = ctx.enter_context(tc.tile_pool(name="hidden", bufs=3))
+        mx_pool = ctx.enter_context(tc.tile_pool(name="mx", bufs=2))
+        image_pool = ctx.enter_context(tc.tile_pool(name="image", bufs=2))
+        psum_spread = ctx.enter_context(tc.psum_pool(name="psum_spread", bufs=4))
+        psum_acc = ctx.enter_context(tc.psum_pool(name="psum_acc", bufs=4))
+        ctx.enter_context(tc.manual_schedule())
+
+        by_point = coords.rearrange("b x c -> x b c")
+        own_bf = setup.tile([P, BATCH, DIMS], BF16)
+        nc.sync.dma_start(out=own_bf[:], in_=by_point)
+        shifted_bf = setup.tile([P, BATCH, DIMS], BF16)
+        nc.sync.dma_start(out=shifted_bf[0:HALF], in_=by_point[HALF:POINTS])
+        nc.sync.dma_start(out=shifted_bf[HALF:POINTS], in_=by_point[0:HALF])
+        w1_bf = setup.tile([P, PACK], BF16)
+        nc.sync.dma_start(out=w1_bf[:], in_=w1.rearrange("o (p t) -> (o p) t", t=PACK))
+        b1_bf = setup.tile([P, PACK], BF16)
+        nc.sync.dma_start(out=b1_bf[:], in_=b1.rearrange("(p t) -> p t", t=PACK))
+        w2_codes = const.tile([P, HEADS], U32, align_bytes=64)
+        nc.sync.dma_start(
+            out=w2_codes[:].bitcast(I32), in_=w2_words[0].rearrange("p k t -> p (k t)").bitcast(I32)
+        )
+        w2_plane = const.tile([P, HEADS], U8, align_bytes=64)
+        nc.vector.memset(w2_plane[:].bitcast(I32), 0)
+        for quadrant in range(4):
+            nc.sync.dma_start(
+                out=w2_plane[32 * quadrant : 32 * quadrant + 4, :].bitcast(I32),
+                in_=w2_scales[0, 4 * quadrant : 4 * quadrant + 4, :].bitcast(I32),
+            )
+        b2_bf = setup.tile([P, 1], BF16)
+        nc.sync.dma_start(out=b2_bf[:], in_=b2.rearrange("(k o) -> k o", o=1))
+
+        ident = const.tile([P, P], F32)
+        make_identity(nc, ident[:])
+        keep = const.tile([P, 2, HALF], F32)
+        nc.gpsimd.memset(keep[:], 1.0)
+        nc.gpsimd.affine_select(
+            out=keep[:, 0, :], in_=keep[:, 0, :], pattern=[[-1, HALF]], base=0, channel_multiplier=1,
+            compare_op=ALU.is_ge, fill=0.0,
+        )
+        nc.gpsimd.affine_select(
+            out=keep[:, 1, :], in_=keep[:, 1, :], pattern=[[1, HALF]], base=-1, channel_multiplier=-1,
+            compare_op=ALU.is_ge, fill=0.0,
+        )
+
+        points = const.tile([P, DIMS, BATCH, 2], F32)
+        nc.vector.tensor_copy(out=points[:, :, :, 0], in_=own_bf[:].rearrange("p b c -> p c b"))
+        nc.vector.tensor_copy(out=points[:, :, :, 1], in_=shifted_bf[:].rearrange("p b c -> p c b"))
+        w1_col = const.tile([P, PACK], F32)
+        nc.vector.tensor_copy(out=w1_col[:], in_=w1_bf[:])
+        b1_col = const.tile([P, PACK], F32)
+        nc.vector.tensor_copy(out=b1_col[:], in_=b1_bf[:])
+        b2_col = const.tile([P, 1], F32)
+        nc.vector.tensor_copy(out=b2_col[:], in_=b2_bf[:])
+
+        diff = setup.tile([P, DIMS, BATCH, 2, HALF], F32)
+        square = setup.tile([P, DIMS, BATCH, 2, HALF], F32)
+        for c in range(DIMS):
+            spread = psum_spread.tile([P, BATCH, POINTS], F32, tag="spread")
+            for b in range(BATCH):
+                nc.tensor.transpose(spread[:, b, :], points[:, c, b, 0:1].to_broadcast([P, P]), ident[:])
+            nc.vector.tensor_tensor(
+                out=diff[:, c],
+                in0=spread[:].rearrange("p b (h a) -> p b h a", h=2),
+                in1=points[:, c].unsqueeze(3).to_broadcast([P, BATCH, 2, HALF]),
+                op=ALU.subtract,
+            )
+            nc.scalar.activation(out=square[:, c], in_=diff[:, c], func=ACT.Square)
+        both = setup.tile([P, BATCH, 2, HALF], F32)
+        nc.vector.tensor_tensor(out=both[:], in0=square[:, 0], in1=square[:, 1], op=ALU.add)
+        nc.vector.tensor_tensor(out=both[:], in0=both[:], in1=square[:, 2], op=ALU.add)
+        nc.vector.tensor_tensor(
+            out=both[:], in0=both[:], in1=keep[:].unsqueeze(1).to_broadcast([P, BATCH, 2, HALF]), op=ALU.mult
+        )
+        dist_sq = setup.tile([P, BATCH, HALF], F32)
+        nc.vector.tensor_tensor(out=dist_sq[:], in0=both[:, :, 0, :], in1=both[:, :, 1, :], op=ALU.add)
+        dist = const.tile([P, BATCH, HALF], F32)
+        nc.scalar.activation(out=dist[:], in_=dist_sq[:], func=ACT.Sqrt)
+
+        def spread_distances(s):
+            b, g = divmod(s, GROUPS)
+            spread = psum_spread.tile([P, ROWS, POINTS], F32, tag="spread")
+            for r in range(ROWS):
+                a = ROWS * g + r
+                nc.tensor.transpose(spread[:, r, :], dist[:, b, a : a + 1].to_broadcast([P, P]), ident[:])
+            return spread
+
+        def hidden_layer(spread):
+            by_channel = hidden_pool.tile([P, PACK, STEP_PAIRS], BF16)
+            for t in range(PACK):
+                nc.scalar.activation(
+                    out=by_channel[:, t, :], in_=spread[:].rearrange("p r x -> p (r x)"), func=ACT.Silu,
+                    scale=w1_col[:, t : t + 1], bias=b1_col[:, t : t + 1],
+                )
+            return by_channel
+
+        def regroup(by_channel):
+            by_pair = mx_pool.tile([P, STEP_PAIRS, PACK], BF16, align_bytes=64)
+            nc.vector.tensor_copy(
+                out=by_pair[:].rearrange("p (n i) t -> p n t i", i=4),
+                in_=by_channel[:].rearrange("p t (n i) -> p n t i", i=4),
+            )
+            return by_pair
+
+        def quantise(by_pair):
+            codes = mx_pool.tile([P, STEP_PAIRS], U32, align_bytes=64)
+            plane = mx_pool.tile([P, STEP_PAIRS], U8, align_bytes=64)
+            nc.vector.quantize_mx(
+                out=codes[:].bitcast(FP8X4), scales=plane[:], in_=by_pair[:].rearrange("p n t -> p (n t)")
+            )
+            return codes, plane
+
+        def multiply(codes, plane):
+            acc = psum_acc.tile([P, ROWS, POINTS], F32)
+            nc.tensor.matmul_mx(
+                out=acc[:].rearrange("k r x -> k (r x)"),
+                lhsT=w2_codes[:].bitcast(FP8X4), lhsT_scale=w2_plane[:],
+                rhs=codes[:].bitcast(FP8X4), rhs_scale=plane[:],
+                start=True, stop=True,
+            )
+            return acc
+
+        def image_rows(image):
+            return image[:, 0 : POINTS * POINTS].rearrange("k (i j) -> k i j", j=POINTS)
+
+        def vector_writes(g, acc, image):
+            a0 = ROWS * g
+            rows = image_rows(image)
+            by_x = acc[:].rearrange("k r x -> k x r")
+
+            def write(dst, src):
+                nc.vector.tensor_scalar_add(out=dst, in0=src, scalar1=b2_col[:, 0:1])
+
+            write(rows[:, a0 : a0 + ROWS, a0 : POINTS - SCALAR_COLS], acc[:, :, a0 : POINTS - SCALAR_COLS])
+            write(rows[:, a0 + ROWS : POINTS, a0 : a0 + ROWS], by_x[:, a0 + ROWS : POINTS, :])
+            if a0 > 0:
+                write(rows[:, HALF + a0 : HALF + a0 + ROWS, HALF : HALF + a0], acc[:, :, 0:a0])
+            write(rows[:, HALF : HALF + a0 + ROWS, HALF + a0 : HALF + a0 + ROWS], by_x[:, 0 : a0 + ROWS, :])
+
+        def scalar_writes(g, acc, image):
+            a0 = ROWS * g
+            nc.scalar.activation(
+                out=image_rows(image)[:, a0 : a0 + ROWS, POINTS - SCALAR_COLS : POINTS],
+                in_=acc[:, :, POINTS - SCALAR_COLS : POINTS], func=ACT.Identity, bias=b2_col[:, 0:1], scale=1.0,
+            )
+
+        def mirror_blocks(image, first, last):
+            blocks = image[:].rearrange("k (q e) -> k q e", e=BLOCK_PITCH)[:, first:last, :]
+            for r in range(1, ROWS):
+                nc.gpsimd.tensor_copy(
+                    out=blocks[:, :, POINTS * r : POINTS * r + r],
+                    in_=blocks[:, :, r : r + POINTS * (r - 1) + 1 : POINTS],
+                )
+
+        def store(b, image, first_row):
+            nc.sync.dma_start(
+                out=out[b, :, first_row : first_row + STORE_ROWS, :],
+                in_=image_rows(image)[:, first_row : first_row + STORE_ROWS, :],
+            )
+
+        def finish(s, image):
+            b, g = divmod(s, GROUPS)
+            if g % STORE_GROUPS == STORE_GROUPS - 1:
+                mirror_blocks(image, g + 1 - STORE_GROUPS, g + 1)
+                store(b, image, ROWS * (g + 1) - STORE_ROWS)
+            if g == GROUPS - 1:
+                mirror_blocks(image, GROUPS, N_BLOCKS)
+                for first_row in range(HALF, POINTS, STORE_ROWS):
+                    store(b, image, first_row)
+
+        spreads, channels, pairs, quantised, sums, images = {}, {}, {}, {}, {}, {}
+
+        def live(s):
+            return 0 <= s < STEPS
+
+        for tick in range(STEPS + 7):
+            if live(tick):
+                spreads[tick] = spread_distances(tick)
+            if live(tick - 2):
+                channels[tick - 2] = hidden_layer(spreads[tick - 2])
+            if live(tick - 4):
+                quantised[tick - 4] = quantise(pairs[tick - 4])
+                sums[tick - 4] = multiply(*quantised[tick - 4])
+            if live(tick - 3):
+                pairs[tick - 3] = regroup(channels[tick - 3])
+            if live(tick - 5):
+                b, g = divmod(tick - 5, GROUPS)
+                if g == 0:
+                    image = image_pool.tile([P, N_BLOCKS * BLOCK_PITCH], F32)
+                    images[b] = image
+                vector_writes(g, sums[tick - 5], images[b])
+            if live(tick - 6):
+                b, g = divmod(tick - 6, GROUPS)
+                scalar_writes(g, sums[tick - 6], images[b])
+                finish(tick - 6, images[b])

@@ -28,7 +28,7 @@ BLOCK_PITCH = ROWS * POINTS + ROWS
 N_BLOCKS = POINTS // ROWS
 STORE_ROWS = 16
 STORE_GROUPS = STORE_ROWS // ROWS
-SCALAR_COLS = 48
+SCALAR_COLS = 24
 
 FLOPS = 2 * BATCH * POINTS * POINTS * HIDDEN * HEADS
 
@@ -170,17 +170,27 @@ def tile_distancerelativebias_kernel(tc, coords, w1, b1, w2_words, w2_scales, b2
             def write(dst, src):
                 nc.vector.tensor_scalar_add(out=dst, in0=src, scalar1=b2_col[:, 0:1])
 
-            write(rows[:, a0 : a0 + ROWS, a0 : POINTS - SCALAR_COLS], acc[:, :, a0 : POINTS - SCALAR_COLS])
-            write(rows[:, a0 + ROWS : POINTS, a0 : a0 + ROWS], by_x[:, a0 + ROWS : POINTS, :])
+            write(rows[:, HALF : HALF + a0 + ROWS, HALF + a0 : HALF + a0 + ROWS], by_x[:, 0 : a0 + ROWS, :])
             if a0 > 0:
                 write(rows[:, HALF + a0 : HALF + a0 + ROWS, HALF : HALF + a0], acc[:, :, 0:a0])
-            write(rows[:, HALF : HALF + a0 + ROWS, HALF + a0 : HALF + a0 + ROWS], by_x[:, 0 : a0 + ROWS, :])
+            if a0 + ROWS < HALF:
+                write(rows[:, a0 + ROWS : HALF, a0 : a0 + ROWS], by_x[:, a0 + ROWS : HALF, :])
+            write(rows[:, a0 : a0 + ROWS, a0 : POINTS - SCALAR_COLS], acc[:, :, a0 : POINTS - SCALAR_COLS])
 
         def scalar_writes(g, acc, image):
             a0 = ROWS * g
             nc.scalar.activation(
                 out=image_rows(image)[:, a0 : a0 + ROWS, POINTS - SCALAR_COLS : POINTS],
                 in_=acc[:, :, POINTS - SCALAR_COLS : POINTS], func=ACT.Identity, bias=b2_col[:, 0:1], scale=1.0,
+            )
+
+        def mirror_quadrant(g, image):
+            a0 = ROWS * g
+            rows = image_rows(image)
+            nc.gpsimd.tensor_scalar(
+                out=rows[:, HALF:POINTS, a0 : a0 + ROWS],
+                in0=rows[:, a0 : a0 + ROWS, HALF:POINTS].rearrange("k r x -> k x r"),
+                scalar1=1.0, scalar2=0.0, op0=ALU.mult, op1=ALU.add,
             )
 
         def mirror_blocks(image, first, last):
@@ -217,18 +227,19 @@ def tile_distancerelativebias_kernel(tc, coords, w1, b1, w2_words, w2_scales, b2
                 spreads[tick] = spread_distances(tick)
             if live(tick - 2):
                 channels[tick - 2] = hidden_layer(spreads[tick - 2])
-            if live(tick - 4):
-                quantised[tick - 4] = quantise(pairs[tick - 4])
-                sums[tick - 4] = multiply(*quantised[tick - 4])
-            if live(tick - 3):
-                pairs[tick - 3] = regroup(channels[tick - 3])
             if live(tick - 5):
                 b, g = divmod(tick - 5, GROUPS)
                 if g == 0:
                     image = image_pool.tile([P, N_BLOCKS * BLOCK_PITCH], F32)
                     images[b] = image
-                vector_writes(g, sums[tick - 5], images[b])
+                scalar_writes(g, sums[tick - 5], images[b])
+            if live(tick - 4):
+                quantised[tick - 4] = quantise(pairs[tick - 4])
+                sums[tick - 4] = multiply(*quantised[tick - 4])
+            if live(tick - 3):
+                pairs[tick - 3] = regroup(channels[tick - 3])
             if live(tick - 6):
                 b, g = divmod(tick - 6, GROUPS)
-                scalar_writes(g, sums[tick - 6], images[b])
+                vector_writes(g, sums[tick - 6], images[b])
+                mirror_quadrant(g, images[b])
                 finish(tick - 6, images[b])

@@ -29,6 +29,12 @@ N_BLOCKS = POINTS // ROWS
 STORE_ROWS = 16
 STORE_GROUPS = STORE_ROWS // ROWS
 SCALAR_COLS = 24
+MADE_FROM = 9
+
+
+def has_made_row(s):
+    return s % 2 == 1 and s >= MADE_FROM
+
 
 FLOPS = 2 * BATCH * POINTS * POINTS * HIDDEN * HEADS
 
@@ -39,6 +45,7 @@ def tile_distancerelativebias_kernel(tc, coords, w1, b1, w2_words, w2_scales, b2
         const = ctx.enter_context(tc.tile_pool(name="const", bufs=1))
         setup = ctx.enter_context(tc.tile_pool(name="setup", bufs=1))
         hidden_pool = ctx.enter_context(tc.tile_pool(name="hidden", bufs=3))
+        pair_pool = ctx.enter_context(tc.tile_pool(name="pair", bufs=3))
         mx_pool = ctx.enter_context(tc.tile_pool(name="mx", bufs=2))
         image_pool = ctx.enter_context(tc.tile_pool(name="image", bufs=2))
         psum_spread = ctx.enter_context(tc.psum_pool(name="psum_spread", bufs=4))
@@ -66,6 +73,9 @@ def tile_distancerelativebias_kernel(tc, coords, w1, b1, w2_words, w2_scales, b2
                 out=w2_plane[32 * quadrant : 32 * quadrant + 4, :].bitcast(I32),
                 in_=w2_scales[0, 4 * quadrant : 4 * quadrant + 4, :].bitcast(I32),
             )
+        rows_bf = setup.tile([P, HIDDEN], BF16)
+        nc.sync.dma_start(out=rows_bf[0:1, :], in_=w1)
+        nc.sync.dma_start(out=rows_bf[32:33, :], in_=b1.rearrange("(o c) -> o c", o=1))
         b2_bf = setup.tile([P, 1], BF16)
         nc.sync.dma_start(out=b2_bf[:], in_=b2.rearrange("(k o) -> k o", o=1))
 
@@ -81,6 +91,12 @@ def tile_distancerelativebias_kernel(tc, coords, w1, b1, w2_words, w2_scales, b2
             out=keep[:, 1, :], in_=keep[:, 1, :], pattern=[[1, HALF]], base=-1, channel_multiplier=-1,
             compare_op=ALU.is_ge, fill=0.0,
         )
+
+        first_layer = const.tile([P, PACK, P], F32)
+        nc.gpsimd.memset(first_layer[:], 0.0)
+        made_rows = const.tile([P, STEPS // 2, POINTS], F32)
+        nc.gpsimd.memset(made_rows[:], 0.0)
+        nc.gpsimd.memset(made_rows[32:33, :, :], 1.0)
 
         points = const.tile([P, DIMS, BATCH, 2], F32)
         nc.vector.tensor_copy(out=points[:, :, :, 0], in_=own_bf[:].rearrange("p b c -> p c b"))
@@ -116,28 +132,61 @@ def tile_distancerelativebias_kernel(tc, coords, w1, b1, w2_words, w2_scales, b2
         dist = const.tile([P, BATCH, HALF], F32)
         nc.scalar.activation(out=dist[:], in_=dist_sq[:], func=ACT.Sqrt)
 
+        for row in (0, 32):
+            nc.vector.tensor_copy(
+                out=first_layer[row : row + 1], in_=rows_bf[row : row + 1, :].rearrange("o (m t) -> o t m", t=PACK)
+            )
+        table_ps = psum_spread.tile([P, 2, POINTS], F32, tag="spread")
+        for h in range(2):
+            nc.tensor.transpose(
+                table_ps[:, h, :], dist[:, 2 * h : 2 * h + 2, :].rearrange("x b a -> x (b a)"), ident[:]
+            )
+        table_sb = setup.tile([P, 2, POINTS], F32)
+        nc.vector.tensor_copy(out=table_sb[:], in_=table_ps[:])
+        parked = out[BATCH - 1, HEADS - 2 : HEADS, :, :]
+        nc.sync.dma_start(out=parked.rearrange("h q x -> q h x"), in_=table_sb[:])
+        nc.sync.dma_start(
+            out=made_rows[0:1, :, :],
+            in_=parked.rearrange("h (u r) x -> h u r x", r=2 * ROWS)[:, :, 2 * ROWS - 1, :]
+            .rearrange("h u x -> (h u) x")
+            .unsqueeze(0),
+        )
+
         def spread_distances(s):
             b, g = divmod(s, GROUPS)
             spread = psum_spread.tile([P, ROWS, POINTS], F32, tag="spread")
-            for r in range(ROWS):
+            for r in range(ROWS - 1 if has_made_row(s) else ROWS):
                 a = ROWS * g + r
                 nc.tensor.transpose(spread[:, r, :], dist[:, b, a : a + 1].to_broadcast([P, P]), ident[:])
-            return spread
+            if not has_made_row(s):
+                return spread, None
+            made = psum_spread.tile([P, POINTS, PACK], F32, tag="spread")
+            for t in range(PACK):
+                nc.tensor.matmul(
+                    out=made[:, :, t], lhsT=first_layer[:, t, :], rhs=made_rows[:, s // 2, :], start=True, stop=True
+                )
+            return spread, made
 
-        def hidden_layer(spread):
+        def hidden_layer(spread, made):
+            rows = ROWS if made is None else ROWS - 1
             by_channel = hidden_pool.tile([P, PACK, STEP_PAIRS], BF16)
+            by_pair = pair_pool.tile([P, STEP_PAIRS, PACK], BF16, align_bytes=64)
             for t in range(PACK):
                 nc.scalar.activation(
-                    out=by_channel[:, t, :], in_=spread[:].rearrange("p r x -> p (r x)"), func=ACT.Silu,
-                    scale=w1_col[:, t : t + 1], bias=b1_col[:, t : t + 1],
+                    out=by_channel[:, t, 0 : rows * POINTS], in_=spread[:, 0:rows, :].rearrange("p r x -> p (r x)"),
+                    func=ACT.Silu, scale=w1_col[:, t : t + 1], bias=b1_col[:, t : t + 1],
                 )
-            return by_channel
+            if made is not None:
+                nc.scalar.activation(
+                    out=by_pair[:, rows * POINTS : STEP_PAIRS, :].rearrange("p n t -> p (n t)"),
+                    in_=made[:].rearrange("p n t -> p (n t)"), func=ACT.Silu,
+                )
+            return by_channel, by_pair, rows * POINTS
 
-        def regroup(by_channel):
-            by_pair = mx_pool.tile([P, STEP_PAIRS, PACK], BF16, align_bytes=64)
+        def regroup(by_channel, by_pair, count):
             nc.vector.tensor_copy(
-                out=by_pair[:].rearrange("p (n i) t -> p n t i", i=4),
-                in_=by_channel[:].rearrange("p t (n i) -> p n t i", i=4),
+                out=by_pair[:, 0:count, :].rearrange("p (n i) t -> p n t i", i=4),
+                in_=by_channel[:, :, 0:count].rearrange("p t (n i) -> p n t i", i=4),
             )
             return by_pair
 
@@ -226,7 +275,7 @@ def tile_distancerelativebias_kernel(tc, coords, w1, b1, w2_words, w2_scales, b2
             if live(tick):
                 spreads[tick] = spread_distances(tick)
             if live(tick - 2):
-                channels[tick - 2] = hidden_layer(spreads[tick - 2])
+                channels[tick - 2] = hidden_layer(*spreads[tick - 2])
             if live(tick - 5):
                 b, g = divmod(tick - 5, GROUPS)
                 if g == 0:
@@ -237,7 +286,7 @@ def tile_distancerelativebias_kernel(tc, coords, w1, b1, w2_words, w2_scales, b2
                 quantised[tick - 4] = quantise(pairs[tick - 4])
                 sums[tick - 4] = multiply(*quantised[tick - 4])
             if live(tick - 3):
-                pairs[tick - 3] = regroup(channels[tick - 3])
+                pairs[tick - 3] = regroup(*channels[tick - 3])
             if live(tick - 6):
                 b, g = divmod(tick - 6, GROUPS)
                 vector_writes(g, sums[tick - 6], images[b])

@@ -52,6 +52,10 @@ def tile_distancerelativebias_kernel(tc, coords, w1, b1, w2_words, w2_scales, b2
         psum_acc = ctx.enter_context(tc.psum_pool(name="psum_acc", bufs=4))
         ctx.enter_context(tc.manual_schedule())
 
+        warm = setup.tile([P, 1], F32)
+        nc.vector.memset(warm[:], 1.0)
+        nc.scalar.activation(out=warm[:], in_=warm[:], func=ACT.Sqrt)
+
         by_point = coords.rearrange("b x c -> x b c")
         own_bf = setup.tile([P, BATCH, DIMS], BF16)
         nc.sync.dma_start(out=own_bf[:], in_=by_point)
@@ -243,28 +247,31 @@ def tile_distancerelativebias_kernel(tc, coords, w1, b1, w2_words, w2_scales, b2
             )
 
         def mirror_blocks(image, first, last):
-            blocks = image[:].rearrange("k (q e) -> k q e", e=BLOCK_PITCH)[:, first:last, :]
+            blocks = image[:].rearrange("k (h q e) -> k h q e", h=2, e=BLOCK_PITCH)[:, :, first:last, :]
             for r in range(1, ROWS):
                 nc.gpsimd.tensor_copy(
-                    out=blocks[:, :, POINTS * r : POINTS * r + r],
-                    in_=blocks[:, :, r : r + POINTS * (r - 1) + 1 : POINTS],
+                    out=blocks[:, :, :, POINTS * r : POINTS * r + r],
+                    in_=blocks[:, :, :, r : r + POINTS * (r - 1) + 1 : POINTS],
                 )
 
-        def store(b, image, first_row):
+        def store(b, image, first_row, count):
             nc.sync.dma_start(
-                out=out[b, :, first_row : first_row + STORE_ROWS, :],
-                in_=image_rows(image)[:, first_row : first_row + STORE_ROWS, :],
+                out=out[b, :, first_row : first_row + count, :],
+                in_=image_rows(image)[:, first_row : first_row + count, :],
             )
 
         def finish(s, image):
             b, g = divmod(s, GROUPS)
-            if g % STORE_GROUPS == STORE_GROUPS - 1:
+            if s >= STEPS - STORE_GROUPS:
+                if g % 2 == 1:
+                    mirror_blocks(image, g - 1, g + 1)
+                    store(b, image, ROWS * (g - 1), 2 * ROWS)
+            elif g % STORE_GROUPS == STORE_GROUPS - 1:
                 mirror_blocks(image, g + 1 - STORE_GROUPS, g + 1)
-                store(b, image, ROWS * (g + 1) - STORE_ROWS)
+                store(b, image, ROWS * (g + 1) - STORE_ROWS, STORE_ROWS)
             if g == GROUPS - 1:
-                mirror_blocks(image, GROUPS, N_BLOCKS)
                 for first_row in range(HALF, POINTS, STORE_ROWS):
-                    store(b, image, first_row)
+                    store(b, image, first_row, STORE_ROWS)
 
         spreads, channels, pairs, quantised, sums, images = {}, {}, {}, {}, {}, {}
 

@@ -189,8 +189,8 @@ def tile_distancerelativebias_kernel(tc, coords, w1, b1, w2_words, w2_scales, b2
 
         def regroup(by_channel, by_pair, count):
             nc.vector.tensor_copy(
-                out=by_pair[:, 0:count, :].rearrange("p (n i) t -> p n t i", i=4),
-                in_=by_channel[:, :, 0:count].rearrange("p t (n i) -> p n t i", i=4),
+                out=by_pair[:, 0:count, :].rearrange("p (n i) t -> p n t i", i=8),
+                in_=by_channel[:, :, 0:count].rearrange("p t (n i) -> p n t i", i=8),
             )
             return by_pair
 

@@ -189,8 +189,8 @@ def tile_distancerelativebias_kernel(tc, coords, w1, b1, w2_words, w2_scales, b2
 
         def regroup(by_channel, by_pair, count):
             nc.vector.tensor_copy(
-                out=by_pair[:, 0:count, :].rearrange("p (n i) t -> p n t i", i=8),
-                in_=by_channel[:, :, 0:count].rearrange("p t (n i) -> p n t i", i=8),
+                out=by_pair[:, 0:count, :].rearrange("p (n i) t -> p n t i", i=2),
+                in_=by_channel[:, :, 0:count].rearrange("p t (n i) -> p n t i", i=2),
             )
             return by_pair
 

@@ -164,10 +164,10 @@ def tile_distancerelativebias_kernel(tc, coords, w1, b1, w2_words, w2_scales, b2
                 nc.tensor.transpose(spread[:, r, :], dist[:, b, a : a + 1].to_broadcast([P, P]), ident[:])
             if not has_made_row(s):
                 return spread, None
-            made = psum_spread.tile([P, POINTS, PACK], F32, tag="spread")
+            made = psum_spread.tile([P, PACK, POINTS], F32, tag="spread")
             for t in range(PACK):
                 nc.tensor.matmul(
-                    out=made[:, :, t], lhsT=first_layer[:, t, :], rhs=made_rows[:, s // 2, :], start=True, stop=True
+                    out=made[:, t, :], lhsT=first_layer[:, t, :], rhs=made_rows[:, s // 2, :], start=True, stop=True
                 )
             return spread, made
 
@@ -182,8 +182,8 @@ def tile_distancerelativebias_kernel(tc, coords, w1, b1, w2_words, w2_scales, b2
                 )
             if made is not None:
                 nc.scalar.activation(
-                    out=by_pair[:, rows * POINTS : STEP_PAIRS, :].rearrange("p n t -> p (n t)"),
-                    in_=made[:].rearrange("p n t -> p (n t)"), func=ACT.Silu,
+                    out=by_pair[:, rows * POINTS : STEP_PAIRS, :],
+                    in_=made[:].rearrange("p t n -> p n t"), func=ACT.Silu,
                 )
             return by_channel, by_pair, rows * POINTS
 

@@ -23,18 +23,55 @@ PACK = 4
 ROWS = 4
 STEP_PAIRS = ROWS * POINTS
 GROUPS = HALF // ROWS
-STEPS = BATCH * GROUPS
-BLOCK_PITCH = ROWS * POINTS + ROWS
-N_BLOCKS = POINTS // ROWS
 STORE_ROWS = 16
 STORE_GROUPS = STORE_ROWS // ROWS
+POINT_PITCH = 16
+LAST = BATCH - 1
+LAST_FROM = LAST * GROUPS
+BLOCK = 16
+CELL = 8
+FOLDS = [(i, 2 * i + h) for i in range(4) for h in range(2)]
+STRIPS = (
+    [(i, m) for i in range(4) for m in range(2 * i + 2, 16)]
+    + [(i, 2 * j + h) for j in range(3) for i in range(j + 1, 4) for h in range(2)]
+)
+FOLD_STEPS = len(FOLDS) // 2
+IN_ORDER = STRIPS[2 * FOLD_STEPS :]
+LAST_STEPS = (
+    [FOLDS[2 * n : 2 * n + 2] + STRIPS[2 * n : 2 * n + 2] for n in range(FOLD_STEPS)]
+    + [IN_ORDER[n : n + ROWS] for n in range(0, len(IN_ORDER) - ROWS, ROWS)]
+    + [IN_ORDER[-4:-2], IN_ORDER[-2:]]
+)
+STRIPS_FROM = LAST_FROM + FOLD_STEPS
+STEPS = LAST_FROM + len(LAST_STEPS)
+COMPLETE = {53: [0], 56: [1], 58: [2], 60: [3], 62: [4], 63: [5], 64: [6, 7]}
 SCALAR_COLS = 24
-MADE_FROM = 9
+SCALAR_ALONE_FROM = STEPS - 4
+MADE = range(7, 62, 2)
+
+
+LAST_DIST_TICK = 12
 
 
 def has_made_row(s):
-    return s % 2 == 1 and s >= MADE_FROM
+    return s in MADE
 
+
+def table_rows(s):
+    return ROWS if s < LAST_FROM else len(LAST_STEPS[s - LAST_FROM])
+
+
+def segments(cells):
+    runs = []
+    for n, (i, m) in enumerate(cells):
+        if runs and runs[-1][1] == i and runs[-1][2] + runs[-1][3] == m:
+            runs[-1] = runs[-1][:3] + (runs[-1][3] + 1,)
+        else:
+            runs.append((n, i, m, 1))
+    return runs
+
+
+IMAGE = POINTS * POINTS + POINTS
 
 FLOPS = 2 * BATCH * POINTS * POINTS * HIDDEN * HEADS
 
@@ -57,11 +94,11 @@ def tile_distancerelativebias_kernel(tc, coords, w1, b1, w2_words, w2_scales, b2
         nc.scalar.activation(out=warm[:], in_=warm[:], func=ACT.Sqrt)
 
         by_point = coords.rearrange("b x c -> x b c")
-        own_bf = setup.tile([P, BATCH, DIMS], BF16)
-        nc.sync.dma_start(out=own_bf[:], in_=by_point)
-        shifted_bf = setup.tile([P, BATCH, DIMS], BF16)
-        nc.sync.dma_start(out=shifted_bf[0:HALF], in_=by_point[HALF:POINTS])
-        nc.sync.dma_start(out=shifted_bf[HALF:POINTS], in_=by_point[0:HALF])
+        points = setup.tile([P, 2, POINT_PITCH], BF16)
+        by_batch = points[:, :, 0 : BATCH * DIMS].rearrange("x h (b c) -> x b h c", c=DIMS)
+        nc.sync.dma_start(out=by_batch[:, :, 0, :], in_=by_point)
+        nc.sync.dma_start(out=by_batch[0:HALF, :, 1, :], in_=by_point[HALF:POINTS])
+        nc.sync.dma_start(out=by_batch[HALF:POINTS, :, 1, :], in_=by_point[0:HALF])
         w1_bf = setup.tile([P, PACK], BF16)
         nc.sync.dma_start(out=w1_bf[:], in_=w1.rearrange("o (p t) -> (o p) t", t=PACK))
         b1_bf = setup.tile([P, PACK], BF16)
@@ -83,8 +120,8 @@ def tile_distancerelativebias_kernel(tc, coords, w1, b1, w2_words, w2_scales, b2
         b2_bf = setup.tile([P, 1], BF16)
         nc.sync.dma_start(out=b2_bf[:], in_=b2.rearrange("(k o) -> k o", o=1))
 
-        ident = const.tile([P, P], F32)
-        make_identity(nc, ident[:])
+        ident_bf = setup.tile([P, P], BF16)
+        make_identity(nc, ident_bf[:])
         keep = const.tile([P, 2, HALF], F32)
         nc.gpsimd.memset(keep[:], 1.0)
         nc.gpsimd.affine_select(
@@ -96,46 +133,50 @@ def tile_distancerelativebias_kernel(tc, coords, w1, b1, w2_words, w2_scales, b2
             compare_op=ALU.is_ge, fill=0.0,
         )
 
+        ident = const.tile([P, P], F32)
+        make_identity(nc, ident[:])
+
         first_layer = const.tile([P, PACK, P], F32)
         nc.gpsimd.memset(first_layer[:], 0.0)
         made_rows = const.tile([P, STEPS // 2, POINTS], F32)
         nc.gpsimd.memset(made_rows[:], 0.0)
         nc.gpsimd.memset(made_rows[32:33, :, :], 1.0)
 
-        points = const.tile([P, DIMS, BATCH, 2], F32)
-        nc.vector.tensor_copy(out=points[:, :, :, 0], in_=own_bf[:].rearrange("p b c -> p c b"))
-        nc.vector.tensor_copy(out=points[:, :, :, 1], in_=shifted_bf[:].rearrange("p b c -> p c b"))
+        diff = setup.tile([P, DIMS, BATCH, 2, HALF], F32)
+        square = setup.tile([P, DIMS, BATCH, 2, HALF], F32)
+        for c in range(DIMS):
+            spread = psum_spread.tile([P, BATCH, POINTS], BF16, tag="spread")
+            for b in range(BATCH):
+                column = points[:, 0, DIMS * b + c : DIMS * b + c + 1]
+                nc.tensor.transpose(spread[:, b, :], column.to_broadcast([P, P]), ident_bf[:])
+            nc.vector.tensor_tensor(
+                out=diff[:, c],
+                in0=spread[:].rearrange("p b (h a) -> p b h a", h=2),
+                in1=by_batch[:, :, :, c].unsqueeze(3).to_broadcast([P, BATCH, 2, HALF]),
+                op=ALU.subtract,
+            )
+            nc.scalar.activation(out=square[:, c], in_=diff[:, c], func=ACT.Square)
         w1_col = const.tile([P, PACK], F32)
         nc.vector.tensor_copy(out=w1_col[:], in_=w1_bf[:])
         b1_col = const.tile([P, PACK], F32)
         nc.vector.tensor_copy(out=b1_col[:], in_=b1_bf[:])
+        both = setup.tile([P, BATCH, 2, HALF], F32)
+        dist_sq = setup.tile([P, BATCH, HALF], F32)
+        dist = const.tile([P, BATCH, HALF], F32)
+        halves = (slice(0, BATCH // 2), slice(BATCH // 2, BATCH))
+        for h in halves:
+            nc.vector.tensor_tensor(out=both[:, h], in0=square[:, 0, h], in1=square[:, 1, h], op=ALU.add)
+        for h in halves:
+            nc.vector.tensor_tensor(out=both[:, h], in0=both[:, h], in1=square[:, 2, h], op=ALU.add)
+        keep_both = keep[:].unsqueeze(1).to_broadcast([P, BATCH // 2, 2, HALF])
+        for h in halves:
+            nc.vector.tensor_tensor(out=both[:, h], in0=both[:, h], in1=keep_both, op=ALU.mult)
+        for h in halves:
+            nc.vector.tensor_tensor(out=dist_sq[:, h], in0=both[:, h, 0, :], in1=both[:, h, 1, :], op=ALU.add)
+            nc.scalar.activation(out=dist[:, h], in_=dist_sq[:, h], func=ACT.Sqrt)
+
         b2_col = const.tile([P, 1], F32)
         nc.vector.tensor_copy(out=b2_col[:], in_=b2_bf[:])
-
-        diff = setup.tile([P, DIMS, BATCH, 2, HALF], F32)
-        square = setup.tile([P, DIMS, BATCH, 2, HALF], F32)
-        for c in range(DIMS):
-            spread = psum_spread.tile([P, BATCH, POINTS], F32, tag="spread")
-            for b in range(BATCH):
-                nc.tensor.transpose(spread[:, b, :], points[:, c, b, 0:1].to_broadcast([P, P]), ident[:])
-            nc.vector.tensor_tensor(
-                out=diff[:, c],
-                in0=spread[:].rearrange("p b (h a) -> p b h a", h=2),
-                in1=points[:, c].unsqueeze(3).to_broadcast([P, BATCH, 2, HALF]),
-                op=ALU.subtract,
-            )
-            nc.scalar.activation(out=square[:, c], in_=diff[:, c], func=ACT.Square)
-        both = setup.tile([P, BATCH, 2, HALF], F32)
-        nc.vector.tensor_tensor(out=both[:], in0=square[:, 0], in1=square[:, 1], op=ALU.add)
-        nc.vector.tensor_tensor(out=both[:], in0=both[:], in1=square[:, 2], op=ALU.add)
-        nc.vector.tensor_tensor(
-            out=both[:], in0=both[:], in1=keep[:].unsqueeze(1).to_broadcast([P, BATCH, 2, HALF]), op=ALU.mult
-        )
-        dist_sq = setup.tile([P, BATCH, HALF], F32)
-        nc.vector.tensor_tensor(out=dist_sq[:], in0=both[:, :, 0, :], in1=both[:, :, 1, :], op=ALU.add)
-        dist = const.tile([P, BATCH, HALF], F32)
-        nc.scalar.activation(out=dist[:], in_=dist_sq[:], func=ACT.Sqrt)
-
         for row in (0, 32):
             nc.vector.tensor_copy(
                 out=first_layer[row : row + 1], in_=rows_bf[row : row + 1, :].rearrange("o (m t) -> o t m", t=PACK)
@@ -147,21 +188,41 @@ def tile_distancerelativebias_kernel(tc, coords, w1, b1, w2_words, w2_scales, b2
             )
         table_sb = setup.tile([P, 2, POINTS], F32)
         nc.vector.tensor_copy(out=table_sb[:], in_=table_ps[:])
-        parked = out[BATCH - 1, HEADS - 2 : HEADS, :, :]
+        parked = out[LAST, HEADS - 2 : HEADS, :, :]
         nc.sync.dma_start(out=parked.rearrange("h q x -> q h x"), in_=table_sb[:])
+        first_batches = parked.rearrange("h q x -> (h q) x")[0 : LAST * HALF, :]
         nc.sync.dma_start(
-            out=made_rows[0:1, :, :],
-            in_=parked.rearrange("h (u r) x -> h u r x", r=2 * ROWS)[:, :, 2 * ROWS - 1, :]
-            .rearrange("h u x -> (h u) x")
-            .unsqueeze(0),
+            out=made_rows[0:1, 0 : LAST_FROM // 2, :],
+            in_=first_batches.rearrange("(u r) x -> u r x", r=2 * ROWS)[:, 2 * ROWS - 1, :].unsqueeze(0),
         )
+        blocked = out[LAST, HEADS - 3, 0:HALF, :]
+        for i in range(HALF // BLOCK):
+            nc.sync.dma_start(
+                out=blocked[BLOCK * i : BLOCK * (i + 1), :].rearrange("m (a x) -> a m x", x=CELL),
+                in_=table_sb[HALF + BLOCK * i : HALF + BLOCK * (i + 1), 1, :].rearrange("a (m x) -> a m x", x=CELL),
+            )
+        last_rows = setup.tile([P, POINTS], F32)
+        nc.gpsimd.memset(last_rows[:], 0.0)
+        nc.sync.dma_start(out=last_rows[0:HALF, :], in_=blocked)
+        for s in MADE:
+            if s >= LAST_FROM:
+                i, m = LAST_STEPS[s - LAST_FROM][ROWS - 1]
+                row = BLOCK * i + m
+                nc.sync.dma_start(out=made_rows[0:1, s // 2, :], in_=blocked[row : row + 1, :])
+        last_dist = const.tile([P, HALF], F32)
+
+        def run_of_pairs(s, r):
+            if s < LAST_FROM:
+                b, g = divmod(s, GROUPS)
+                return dist[:, b, ROWS * g + r : ROWS * g + r + 1]
+            i, m = LAST_STEPS[s - LAST_FROM][r]
+            return last_dist[:, BLOCK * i + m : BLOCK * i + m + 1]
 
         def spread_distances(s):
-            b, g = divmod(s, GROUPS)
+            count = table_rows(s) - (1 if has_made_row(s) else 0)
             spread = psum_spread.tile([P, ROWS, POINTS], F32, tag="spread")
-            for r in range(ROWS - 1 if has_made_row(s) else ROWS):
-                a = ROWS * g + r
-                nc.tensor.transpose(spread[:, r, :], dist[:, b, a : a + 1].to_broadcast([P, P]), ident[:])
+            for r in range(count):
+                nc.tensor.transpose(spread[:, r, :], run_of_pairs(s, r).to_broadcast([P, P]), ident[:])
             if not has_made_row(s):
                 return spread, None
             made = psum_spread.tile([P, PACK, POINTS], F32, tag="spread")
@@ -171,84 +232,161 @@ def tile_distancerelativebias_kernel(tc, coords, w1, b1, w2_words, w2_scales, b2
                 )
             return spread, made
 
-        def hidden_layer(spread, made):
-            rows = ROWS if made is None else ROWS - 1
+        def parts(s, count):
+            return [(0, count // 2), (count // 2, count)] if s == 0 else [(0, count)]
+
+        def hidden_layer(s, spread, made):
+            count = POINTS * (table_rows(s) - (0 if made is None else 1))
             by_channel = hidden_pool.tile([P, PACK, STEP_PAIRS], BF16)
             by_pair = pair_pool.tile([P, STEP_PAIRS, PACK], BF16, align_bytes=64)
-            for t in range(PACK):
-                nc.scalar.activation(
-                    out=by_channel[:, t, 0 : rows * POINTS], in_=spread[:, 0:rows, :].rearrange("p r x -> p (r x)"),
-                    func=ACT.Silu, scale=w1_col[:, t : t + 1], bias=b1_col[:, t : t + 1],
-                )
+            for low, high in parts(s, count):
+                for t in range(PACK):
+                    nc.scalar.activation(
+                        out=by_channel[:, t, low:high], in_=spread[:].rearrange("p r x -> p (r x)")[:, low:high],
+                        func=ACT.Silu, scale=w1_col[:, t : t + 1], bias=b1_col[:, t : t + 1],
+                    )
             if made is not None:
                 nc.scalar.activation(
-                    out=by_pair[:, rows * POINTS : STEP_PAIRS, :],
-                    in_=made[:].rearrange("p t n -> p n t"), func=ACT.Silu,
+                    out=by_pair[:, count : count + POINTS, :], in_=made[:].rearrange("p t n -> p n t"), func=ACT.Silu
                 )
-            return by_channel, by_pair, rows * POINTS
+            return by_channel, by_pair, count
 
-        def regroup(by_channel, by_pair, count):
-            nc.vector.tensor_copy(
-                out=by_pair[:, 0:count, :].rearrange("p (n i) t -> p n t i", i=2),
-                in_=by_channel[:, :, 0:count].rearrange("p t (n i) -> p n t i", i=2),
-            )
+        def regroup(s, by_channel, by_pair, count):
+            for low, high in parts(s, count):
+                nc.vector.tensor_copy(
+                    out=by_pair[:, low:high, :].rearrange("p (n i) t -> p n t i", i=2),
+                    in_=by_channel[:, :, low:high].rearrange("p t (n i) -> p n t i", i=2),
+                )
             return by_pair
 
-        def quantise(by_pair):
+        def quantise(s, by_pair):
+            count = POINTS * table_rows(s)
             codes = mx_pool.tile([P, STEP_PAIRS], U32, align_bytes=64)
             plane = mx_pool.tile([P, STEP_PAIRS], U8, align_bytes=64)
             nc.vector.quantize_mx(
-                out=codes[:].bitcast(FP8X4), scales=plane[:], in_=by_pair[:].rearrange("p n t -> p (n t)")
+                out=codes[:, 0:count].bitcast(FP8X4), scales=plane[:, 0:count],
+                in_=by_pair[:, 0:count, :].rearrange("p n t -> p (n t)"),
             )
-            return codes, plane
+            return codes, plane, count
 
-        def multiply(codes, plane):
-            acc = psum_acc.tile([P, ROWS, POINTS], F32)
+        def multiply(codes, plane, count):
+            acc = psum_acc.tile([P, STEP_PAIRS], F32)
             nc.tensor.matmul_mx(
-                out=acc[:].rearrange("k r x -> k (r x)"),
+                out=acc[:, 0:count],
                 lhsT=w2_codes[:].bitcast(FP8X4), lhsT_scale=w2_plane[:],
-                rhs=codes[:].bitcast(FP8X4), rhs_scale=plane[:],
+                rhs=codes[:, 0:count].bitcast(FP8X4), rhs_scale=plane[:, 0:count],
                 start=True, stop=True,
             )
-            return acc
+            return acc[:, 0:count]
 
         def image_rows(image):
             return image[:, 0 : POINTS * POINTS].rearrange("k (i j) -> k i j", j=POINTS)
 
-        def vector_writes(g, acc, image):
-            a0 = ROWS * g
-            rows = image_rows(image)
-            by_x = acc[:].rearrange("k r x -> k x r")
+        def vector_write(dst, src):
+            nc.vector.tensor_scalar_add(out=dst, in0=src, scalar1=b2_col[:, 0:1])
 
-            def write(dst, src):
-                nc.vector.tensor_scalar_add(out=dst, in0=src, scalar1=b2_col[:, 0:1])
+        def scalar_write(dst, src):
+            nc.scalar.activation(out=dst, in_=src, func=ACT.Identity, bias=b2_col[:, 0:1], scale=1.0)
 
-            write(rows[:, HALF : HALF + a0 + ROWS, HALF + a0 : HALF + a0 + ROWS], by_x[:, 0 : a0 + ROWS, :])
-            if a0 > 0:
-                write(rows[:, HALF + a0 : HALF + a0 + ROWS, HALF : HALF + a0], acc[:, :, 0:a0])
-            if a0 + ROWS < HALF:
-                write(rows[:, a0 + ROWS : HALF, a0 : a0 + ROWS], by_x[:, a0 + ROWS : HALF, :])
-            write(rows[:, a0 : a0 + ROWS, a0 : POINTS - SCALAR_COLS], acc[:, :, a0 : POINTS - SCALAR_COLS])
-
-        def scalar_writes(g, acc, image):
-            a0 = ROWS * g
-            nc.scalar.activation(
-                out=image_rows(image)[:, a0 : a0 + ROWS, POINTS - SCALAR_COLS : POINTS],
-                in_=acc[:, :, POINTS - SCALAR_COLS : POINTS], func=ACT.Identity, bias=b2_col[:, 0:1], scale=1.0,
+        def mirror(dst, src):
+            nc.gpsimd.tensor_scalar(
+                out=dst, in0=src.rearrange("k r x -> k x r"), scalar1=1.0, scalar2=0.0, op0=ALU.mult, op1=ALU.add
             )
 
-        def mirror_quadrant(g, image):
+
+        def table_scalar_writes(g, acc, rows):
             a0 = ROWS * g
-            rows = image_rows(image)
+            by_row = acc.rearrange("k (r x) -> k r x", x=POINTS)
+            first = POINTS - SCALAR_COLS
+            scalar_write(rows[:, a0 : a0 + ROWS, first:POINTS], by_row[:, :, first:POINTS])
+
+        def table_vector_writes(g, acc, rows):
+            a0 = ROWS * g
+            a1 = a0 + ROWS
+            by_row = acc.rearrange("k (r x) -> k r x", x=POINTS)
+            by_x = acc.rearrange("k (r x) -> k x r", x=POINTS)
+            vector_write(rows[:, HALF : HALF + a1, HALF + a0 : HALF + a1], by_x[:, 0:a1, :])
+            if a0 > 0:
+                vector_write(rows[:, HALF + a0 : HALF + a1, HALF : HALF + a0], by_row[:, :, 0:a0])
+            if a1 < HALF:
+                vector_write(rows[:, a1:HALF, a0:a1], by_x[:, a1:HALF, :])
+            first = POINTS - SCALAR_COLS
+            vector_write(rows[:, a0:a1, a0:first], by_row[:, :, a0:first])
+            mirror(rows[:, HALF:POINTS, a0:a1], rows[:, a0:a1, HALF:POINTS])
+
+        def place(i, m):
+            if m < 2 * i:
+                return HALF + BLOCK * i, HALF + CELL * m
+            return BLOCK * i, CELL * m
+
+        def first_places(write, acc, rows, cells):
+            for n, i, m, count in segments([cell[1:] for cell in cells]):
+                a0, x0 = place(i, m)
+                c = cells[n][0]
+                write(
+                    rows[:, a0 : a0 + BLOCK, x0 : x0 + CELL * count].rearrange("k a (c x) -> k c a x", x=CELL),
+                    acc[:, POINTS * c : POINTS * (c + count)].rearrange("k (c a x) -> k c a x", a=BLOCK, x=CELL),
+                )
+
+        def second_places(write, acc, rows, cells):
+            for n, i, m, count in segments([cell[1:] for cell in cells]):
+                a0, x0 = place(i, m)
+                c = cells[n][0]
+                write(
+                    rows[:, x0 : x0 + CELL * count, a0 : a0 + BLOCK].rearrange("k (c x) a -> k c x a", x=CELL),
+                    acc[:, POINTS * c : POINTS * (c + count)].rearrange("k (c a x) -> k c x a", a=BLOCK, x=CELL),
+                )
+
+        def strip_shares(s):
+            cells = [(c,) + cell for c, cell in enumerate(LAST_STEPS[s - LAST_FROM])]
+            if s >= STEPS - 2:
+                return cells, [], cells, []
+            if s >= SCALAR_ALONE_FROM:
+                return cells, [], cells[2:], cells[:2]
+            if s < STRIPS_FROM:
+                return cells[3:], cells[2:3], [], cells[2:]
+            return cells[3:], cells[:3], cells[2:], cells[:2]
+
+        def strip_scalar_writes(s, acc, rows):
+            first_places(scalar_write, acc, rows, strip_shares(s)[0])
+
+        def strip_vector_writes(s, acc, rows):
+            scalar_first, vector_first, vector_second, gpsimd_second = strip_shares(s)
+            second_places(vector_write, acc, rows, vector_second)
+            first_places(vector_write, acc, rows, vector_first)
+            for n, i, m, count in segments([cell[1:] for cell in gpsimd_second]):
+                a0, x0 = place(i, m)
+                mirror(
+                    rows[:, x0 : x0 + CELL * count, a0 : a0 + BLOCK], rows[:, a0 : a0 + BLOCK, x0 : x0 + CELL * count]
+                )
+
+        def fold_vector_writes(s, acc, rows):
+            i = LAST_STEPS[s - LAST_FROM][0][0]
+            low, high = BLOCK * i, HALF + BLOCK * i
+            fold = acc[:, 0 : 2 * POINTS]
+            vector_write(
+                rows[:, low : low + BLOCK, low : low + BLOCK].rearrange("k a (c x) -> k c a x", x=CELL),
+                fold.rearrange("k (c a x) -> k c a x", a=BLOCK, x=CELL),
+            )
+            vector_write(
+                rows[:, high : high + BLOCK, high : high + BLOCK].rearrange("k (c x) a -> k c x a", x=CELL),
+                fold.rearrange("k (c a x) -> k c x a", a=BLOCK, x=CELL),
+            )
+
+        def mirror_quarters(image):
+            pitch = BLOCK * POINTS + BLOCK
+            blocks = image[:, 0 : POINTS // BLOCK * pitch].rearrange("k (q e) -> k q e", e=pitch)
+            by_row = blocks[:, :, 0 : BLOCK * POINTS].rearrange("k q (i j) -> k q i j", j=POINTS)
             nc.gpsimd.tensor_scalar(
-                out=rows[:, HALF:POINTS, a0 : a0 + ROWS],
-                in0=rows[:, a0 : a0 + ROWS, HALF:POINTS].rearrange("k r x -> k x r"),
+                out=by_row[:, :, CELL:BLOCK, 0:CELL],
+                in0=by_row[:, :, 0:CELL, CELL:BLOCK].rearrange("k q r x -> k q x r"),
                 scalar1=1.0, scalar2=0.0, op0=ALU.mult, op1=ALU.add,
             )
 
-        def mirror_blocks(image, first, last):
-            blocks = image[:].rearrange("k (h q e) -> k h q e", h=2, e=BLOCK_PITCH)[:, :, first:last, :]
-            for r in range(1, ROWS):
+        def mirror_blocks(image, size, first, last):
+            pitch = size * POINTS + size
+            blocks = image[:].rearrange("k (h q e) -> k h q e", h=2, e=pitch)[:, :, first:last, :]
+            for r in range(1, size):
                 nc.gpsimd.tensor_copy(
                     out=blocks[:, :, :, POINTS * r : POINTS * r + r],
                     in_=blocks[:, :, :, r : r + POINTS * (r - 1) + 1 : POINTS],
@@ -260,42 +398,63 @@ def tile_distancerelativebias_kernel(tc, coords, w1, b1, w2_words, w2_scales, b2
                 in_=image_rows(image)[:, first_row : first_row + count, :],
             )
 
-        def finish(s, image):
-            b, g = divmod(s, GROUPS)
-            if s >= STEPS - STORE_GROUPS:
-                if g % 2 == 1:
-                    mirror_blocks(image, g - 1, g + 1)
-                    store(b, image, ROWS * (g - 1), 2 * ROWS)
-            elif g % STORE_GROUPS == STORE_GROUPS - 1:
-                mirror_blocks(image, g + 1 - STORE_GROUPS, g + 1)
-                store(b, image, ROWS * (g + 1) - STORE_ROWS, STORE_ROWS)
-            if g == GROUPS - 1:
-                for first_row in range(HALF, POINTS, STORE_ROWS):
-                    store(b, image, first_row, STORE_ROWS)
+        def scalar_writes(s, acc, image):
+            rows = image_rows(image)
+            if s < LAST_FROM:
+                table_scalar_writes(s % GROUPS, acc, rows)
+            else:
+                strip_scalar_writes(s, acc, rows)
+
+        def vector_writes(s, acc, image):
+            rows = image_rows(image)
+            if s < LAST_FROM:
+                b, g = divmod(s, GROUPS)
+                table_vector_writes(g, acc, rows)
+                if g % STORE_GROUPS == STORE_GROUPS - 1:
+                    mirror_blocks(image, ROWS, g + 1 - STORE_GROUPS, g + 1)
+                    store(b, image, ROWS * (g + 1) - STORE_ROWS, STORE_ROWS)
+                if g == GROUPS - 1:
+                    for first_row in range(HALF, POINTS, STORE_ROWS):
+                        store(b, image, first_row, STORE_ROWS)
+            else:
+                if s < STRIPS_FROM:
+                    fold_vector_writes(s, acc, rows)
+                strip_vector_writes(s, acc, rows)
+                if s == STRIPS_FROM - 1:
+                    mirror_quarters(image)
+                if s == STRIPS_FROM:
+                    mirror_blocks(image, CELL, 0, HALF // CELL)
+                for n in COMPLETE.get(s, []):
+                    store(LAST, image, STORE_ROWS * n, STORE_ROWS)
 
         spreads, channels, pairs, quantised, sums, images = {}, {}, {}, {}, {}, {}
 
         def live(s):
             return 0 <= s < STEPS
 
+        def batch_of(s):
+            return min(s // GROUPS, LAST)
+
         for tick in range(STEPS + 7):
             if live(tick):
                 spreads[tick] = spread_distances(tick)
             if live(tick - 2):
-                channels[tick - 2] = hidden_layer(*spreads[tick - 2])
+                channels[tick - 2] = hidden_layer(tick - 2, *spreads[tick - 2])
+            if tick == LAST_DIST_TICK + 1:
+                nc.scalar.copy(out=last_dist[:], in_=last_ps[:, 0:HALF])
             if live(tick - 5):
-                b, g = divmod(tick - 5, GROUPS)
-                if g == 0:
-                    image = image_pool.tile([P, N_BLOCKS * BLOCK_PITCH], F32)
+                b = batch_of(tick - 5)
+                if b not in images:
+                    image = image_pool.tile([P, IMAGE], F32)
                     images[b] = image
-                scalar_writes(g, sums[tick - 5], images[b])
+                scalar_writes(tick - 5, sums[tick - 5], images[b])
             if live(tick - 4):
-                quantised[tick - 4] = quantise(pairs[tick - 4])
+                quantised[tick - 4] = quantise(tick - 4, pairs[tick - 4])
                 sums[tick - 4] = multiply(*quantised[tick - 4])
             if live(tick - 3):
-                pairs[tick - 3] = regroup(*channels[tick - 3])
+                pairs[tick - 3] = regroup(tick - 3, *channels[tick - 3])
             if live(tick - 6):
-                b, g = divmod(tick - 6, GROUPS)
-                vector_writes(g, sums[tick - 6], images[b])
-                mirror_quadrant(g, images[b])
-                finish(tick - 6, images[b])
+                vector_writes(tick - 6, sums[tick - 6], images[batch_of(tick - 6)])
+            if tick == LAST_DIST_TICK:
+                last_ps = psum_spread.tile([P, POINTS], F32, tag="spread")
+                nc.tensor.transpose(last_ps[:], last_rows[:], ident[:])

@@ -254,8 +254,8 @@ def tile_distancerelativebias_kernel(tc, coords, w1, b1, w2_words, w2_scales, b2
         def regroup(s, by_channel, by_pair, count):
             for low, high in parts(s, count):
                 nc.vector.tensor_copy(
-                    out=by_pair[:, low:high, :].rearrange("p (n i) t -> p n t i", i=2),
-                    in_=by_channel[:, :, low:high].rearrange("p t (n i) -> p n t i", i=2),
+                    out=by_pair[:, low:high, :].rearrange("p (n i) (u v) -> p n u i v", i=4, u=2),
+                    in_=by_channel[:, :, low:high].rearrange("p (u v) (n i) -> p n u i v", i=4, u=2),
                 )
             return by_pair
 

@@ -24,7 +24,7 @@ ROWS = 4
 STEP_PAIRS = ROWS * POINTS
 GROUPS = HALF // ROWS
 STORE_ROWS = 16
-STORE_GROUPS = STORE_ROWS // ROWS
+MIRROR_GROUPS = GROUPS // 2
 POINT_PITCH = 16
 LAST = BATCH - 1
 LAST_FROM = LAST * GROUPS
@@ -85,8 +85,8 @@ def tile_distancerelativebias_kernel(tc, coords, w1, b1, w2_words, w2_scales, b2
         pair_pool = ctx.enter_context(tc.tile_pool(name="pair", bufs=3))
         mx_pool = ctx.enter_context(tc.tile_pool(name="mx", bufs=2))
         image_pool = ctx.enter_context(tc.tile_pool(name="image", bufs=2))
-        psum_spread = ctx.enter_context(tc.psum_pool(name="psum_spread", bufs=4))
-        psum_acc = ctx.enter_context(tc.psum_pool(name="psum_acc", bufs=4))
+        psum_spread = ctx.enter_context(tc.psum_pool(name="psum_spread", bufs=5))
+        psum_acc = ctx.enter_context(tc.psum_pool(name="psum_acc", bufs=3))
         ctx.enter_context(tc.manual_schedule())
 
         warm = setup.tile([P, 1], F32)
@@ -290,7 +290,8 @@ def tile_distancerelativebias_kernel(tc, coords, w1, b1, w2_words, w2_scales, b2
 
         def mirror(dst, src):
             nc.gpsimd.tensor_scalar(
-                out=dst, in0=src.rearrange("k r x -> k x r"), scalar1=1.0, scalar2=0.0, op0=ALU.mult, op1=ALU.add
+                out=dst.rearrange("k x (n r) -> k n x r", r=4), in0=src.rearrange("k (n r) x -> k n x r", r=4),
+                scalar1=1.0, scalar2=0.0, op0=ALU.mult, op1=ALU.add,
             )
 
 
@@ -387,9 +388,10 @@ def tile_distancerelativebias_kernel(tc, coords, w1, b1, w2_words, w2_scales, b2
             pitch = size * POINTS + size
             blocks = image[:].rearrange("k (h q e) -> k h q e", h=2, e=pitch)[:, :, first:last, :]
             for r in range(1, size):
-                nc.gpsimd.tensor_copy(
+                nc.gpsimd.tensor_scalar(
                     out=blocks[:, :, :, POINTS * r : POINTS * r + r],
-                    in_=blocks[:, :, :, r : r + POINTS * (r - 1) + 1 : POINTS],
+                    in0=blocks[:, :, :, r : r + POINTS * (r - 1) + 1 : POINTS],
+                    scalar1=1.0, scalar2=0.0, op0=ALU.mult, op1=ALU.add,
                 )
 
         def store(b, image, first_row, count):
@@ -410,9 +412,10 @@ def tile_distancerelativebias_kernel(tc, coords, w1, b1, w2_words, w2_scales, b2
             if s < LAST_FROM:
                 b, g = divmod(s, GROUPS)
                 table_vector_writes(g, acc, rows)
-                if g % STORE_GROUPS == STORE_GROUPS - 1:
-                    mirror_blocks(image, ROWS, g + 1 - STORE_GROUPS, g + 1)
-                    store(b, image, ROWS * (g + 1) - STORE_ROWS, STORE_ROWS)
+                if g % MIRROR_GROUPS == MIRROR_GROUPS - 1:
+                    mirror_blocks(image, ROWS, g + 1 - MIRROR_GROUPS, g + 1)
+                    for first_row in range(ROWS * (g + 1 - MIRROR_GROUPS), ROWS * (g + 1), STORE_ROWS):
+                        store(b, image, first_row, STORE_ROWS)
                 if g == GROUPS - 1:
                     for first_row in range(HALF, POINTS, STORE_ROWS):
                         store(b, image, first_row, STORE_ROWS)

@@ -39,15 +39,15 @@ FOLD_STEPS = len(FOLDS) // 2
 IN_ORDER = STRIPS[2 * FOLD_STEPS :]
 LAST_STEPS = (
     [FOLDS[2 * n : 2 * n + 2] + STRIPS[2 * n : 2 * n + 2] for n in range(FOLD_STEPS)]
-    + [IN_ORDER[n : n + ROWS] for n in range(0, len(IN_ORDER) - ROWS, ROWS)]
-    + [IN_ORDER[-4:-2], IN_ORDER[-2:]]
+    + [IN_ORDER[n : n + ROWS] for n in range(0, len(IN_ORDER) - 2 * ROWS, ROWS)]
+    + [IN_ORDER[-8:-6], IN_ORDER[-6:-2], IN_ORDER[-2:]]
 )
 STRIPS_FROM = LAST_FROM + FOLD_STEPS
 STEPS = LAST_FROM + len(LAST_STEPS)
 COMPLETE = {53: [0], 56: [1], 58: [2], 60: [3], 62: [4], 63: [5], 64: [6, 7]}
 SCALAR_COLS = 24
-SCALAR_ALONE_FROM = STEPS - 4
-MADE = range(7, 62, 2)
+SCALAR_ALONE_FROM = STEPS - 5
+MADE = range(9, 64, 2)
 
 
 LAST_DIST_TICK = 12
@@ -81,9 +81,9 @@ def tile_distancerelativebias_kernel(tc, coords, w1, b1, w2_words, w2_scales, b2
     with ExitStack() as ctx:
         const = ctx.enter_context(tc.tile_pool(name="const", bufs=1))
         setup = ctx.enter_context(tc.tile_pool(name="setup", bufs=1))
-        hidden_pool = ctx.enter_context(tc.tile_pool(name="hidden", bufs=3))
+        hidden_pool = ctx.enter_context(tc.tile_pool(name="hidden", bufs=4))
         pair_pool = ctx.enter_context(tc.tile_pool(name="pair", bufs=3))
-        mx_pool = ctx.enter_context(tc.tile_pool(name="mx", bufs=2))
+        mx_pool = ctx.enter_context(tc.tile_pool(name="mx", bufs=3))
         image_pool = ctx.enter_context(tc.tile_pool(name="image", bufs=2))
         psum_spread = ctx.enter_context(tc.psum_pool(name="psum_spread", bufs=5))
         psum_acc = ctx.enter_context(tc.psum_pool(name="psum_acc", bufs=3))
@@ -341,21 +341,26 @@ def tile_distancerelativebias_kernel(tc, coords, w1, b1, w2_words, w2_scales, b2
         def strip_shares(s):
             cells = [(c,) + cell for c, cell in enumerate(LAST_STEPS[s - LAST_FROM])]
             if s >= STEPS - 2:
-                return cells, [], cells, []
+                return cells, [], [], cells, []
             if s >= SCALAR_ALONE_FROM:
-                return cells, [], cells[2:], cells[:2]
+                half = 2 if len(cells) == ROWS else 0
+                return cells, cells[half:], [], [], cells[:half]
+            by_scalar = cells[3:]
+            by_vector = [cell for cell in cells if cell not in by_scalar]
             if s < STRIPS_FROM:
-                return cells[3:], cells[2:3], [], cells[2:]
-            return cells[3:], cells[:3], cells[2:], cells[:2]
+                return by_scalar, [], by_vector[2:], [], cells[2:]
+            return by_scalar, [], by_vector, cells[2:], cells[:2]
 
         def strip_scalar_writes(s, acc, rows):
-            first_places(scalar_write, acc, rows, strip_shares(s)[0])
+            first, second = strip_shares(s)[:2]
+            first_places(scalar_write, acc, rows, first)
+            second_places(scalar_write, acc, rows, second)
 
         def strip_vector_writes(s, acc, rows):
-            scalar_first, vector_first, vector_second, gpsimd_second = strip_shares(s)
-            second_places(vector_write, acc, rows, vector_second)
-            first_places(vector_write, acc, rows, vector_first)
-            for n, i, m, count in segments([cell[1:] for cell in gpsimd_second]):
+            first, second, mirrored = strip_shares(s)[2:]
+            second_places(vector_write, acc, rows, second)
+            first_places(vector_write, acc, rows, first)
+            for n, i, m, count in segments([cell[1:] for cell in mirrored]):
                 a0, x0 = place(i, m)
                 mirror(
                     rows[:, x0 : x0 + CELL * count, a0 : a0 + BLOCK], rows[:, a0 : a0 + BLOCK, x0 : x0 + CELL * count]
@@ -445,12 +450,13 @@ def tile_distancerelativebias_kernel(tc, coords, w1, b1, w2_words, w2_scales, b2
                 channels[tick - 2] = hidden_layer(tick - 2, *spreads[tick - 2])
             if tick == LAST_DIST_TICK + 1:
                 nc.scalar.copy(out=last_dist[:], in_=last_ps[:, 0:HALF])
-            if live(tick - 5):
-                b = batch_of(tick - 5)
-                if b not in images:
-                    image = image_pool.tile([P, IMAGE], F32)
-                    images[b] = image
-                scalar_writes(tick - 5, sums[tick - 5], images[b])
+            if tick - 5 in range(0, STEPS, GROUPS) and tick - 5 <= LAST_FROM:
+                image = image_pool.tile([P, IMAGE], F32)
+                images[batch_of(tick - 5)] = image
+            if tick == STEPS + 1:
+                scalar_writes(SCALAR_ALONE_FROM, sums[SCALAR_ALONE_FROM], images[LAST])
+            if live(tick - 5) and tick - 5 != SCALAR_ALONE_FROM:
+                scalar_writes(tick - 5, sums[tick - 5], images[batch_of(tick - 5)])
             if live(tick - 4):
                 quantised[tick - 4] = quantise(tick - 4, pairs[tick - 4])
                 sums[tick - 4] = multiply(*quantised[tick - 4])

@@ -50,6 +50,8 @@ SCALAR_ALONE_FROM = STEPS - 5
 MADE = range(9, 64, 2)
 
 
+PIECES = 3
+ROUND_TICKS = {7: range(4, 8), 14: range(8, 14), 26: range(14, 20), 38: range(20, 26), 50: range(26, 32)}
 LAST_DIST_TICK = 12
 
 
@@ -115,8 +117,10 @@ def tile_distancerelativebias_kernel(tc, coords, w1, b1, w2_words, w2_scales, b2
                 in_=w2_scales[0, 4 * quadrant : 4 * quadrant + 4, :].bitcast(I32),
             )
         rows_bf = setup.tile([P, HIDDEN], BF16)
-        nc.sync.dma_start(out=rows_bf[0:1, :], in_=w1)
-        nc.sync.dma_start(out=rows_bf[32:33, :], in_=b1.rearrange("(o c) -> o c", o=1))
+        nc.vector.memset(rows_bf[:], 0.0)
+        for piece in range(PIECES):
+            nc.sync.dma_start(out=rows_bf[32 * piece : 32 * piece + 1, :], in_=w1)
+        nc.sync.dma_start(out=rows_bf[96:97, :], in_=b1.rearrange("(o c) -> o c", o=1))
         b2_bf = setup.tile([P, 1], BF16)
         nc.sync.dma_start(out=b2_bf[:], in_=b2.rearrange("(k o) -> k o", o=1))
 
@@ -136,11 +140,11 @@ def tile_distancerelativebias_kernel(tc, coords, w1, b1, w2_words, w2_scales, b2
         ident = const.tile([P, P], F32)
         make_identity(nc, ident[:])
 
-        first_layer = const.tile([P, PACK, P], F32)
-        nc.gpsimd.memset(first_layer[:], 0.0)
-        made_rows = const.tile([P, STEPS // 2, POINTS], F32)
-        nc.gpsimd.memset(made_rows[:], 0.0)
-        nc.gpsimd.memset(made_rows[32:33, :, :], 1.0)
+        first_layer = const.tile([P, PACK, P], BF16)
+        made_rows = const.tile([P, STEPS // 2, POINTS], BF16)
+        piece_rows = setup.tile([P, STEPS // 2, POINTS], F32)
+        nc.gpsimd.memset(piece_rows[:, MADE[0] // 2 :, :], 0.0)
+        nc.gpsimd.memset(piece_rows[96:97, MADE[0] // 2 :, :], 1.0)
 
         diff = setup.tile([P, DIMS, BATCH, 2, HALF], F32)
         square = setup.tile([P, DIMS, BATCH, 2, HALF], F32)
@@ -177,38 +181,45 @@ def tile_distancerelativebias_kernel(tc, coords, w1, b1, w2_words, w2_scales, b2
 
         b2_col = const.tile([P, 1], F32)
         nc.vector.tensor_copy(out=b2_col[:], in_=b2_bf[:])
-        for row in (0, 32):
-            nc.vector.tensor_copy(
-                out=first_layer[row : row + 1], in_=rows_bf[row : row + 1, :].rearrange("o (m t) -> o t m", t=PACK)
-            )
+        nc.vector.tensor_copy(out=first_layer[:], in_=rows_bf[:].rearrange("o (m t) -> o t m", t=PACK))
         table_ps = psum_spread.tile([P, 2, POINTS], F32, tag="spread")
         for h in range(2):
             nc.tensor.transpose(
                 table_ps[:, h, :], dist[:, 2 * h : 2 * h + 2, :].rearrange("x b a -> x (b a)"), ident[:]
             )
-        table_sb = setup.tile([P, 2, POINTS], F32)
-        nc.vector.tensor_copy(out=table_sb[:], in_=table_ps[:])
-        parked = out[LAST, HEADS - 2 : HEADS, :, :]
-        nc.sync.dma_start(out=parked.rearrange("h q x -> q h x"), in_=table_sb[:])
-        first_batches = parked.rearrange("h q x -> (h q) x")[0 : LAST * HALF, :]
+        table_sb = setup.tile([P, PIECES, 2, POINTS], F32)
+        rounded = setup.tile([P, PIECES - 1, 2, POINTS], BF16)
+        nc.vector.tensor_copy(out=table_sb[:, 0], in_=table_ps[:])
+        nc.vector.tensor_copy(out=rounded[:, 0], in_=table_ps[:])
+        nc.vector.tensor_tensor(out=table_sb[:, 1], in0=table_sb[:, 0], in1=rounded[:, 0], op=ALU.subtract)
+        nc.vector.tensor_copy(out=rounded[:, 1], in_=table_sb[:, 1])
+        nc.vector.tensor_tensor(out=table_sb[:, 2], in0=table_sb[:, 1], in1=rounded[:, 1], op=ALU.subtract)
+        parked = out[LAST, HEADS - 2 * PIECES : HEADS, :, :]
         nc.sync.dma_start(
-            out=made_rows[0:1, 0 : LAST_FROM // 2, :],
-            in_=first_batches.rearrange("(u r) x -> u r x", r=2 * ROWS)[:, 2 * ROWS - 1, :].unsqueeze(0),
+            out=parked.rearrange("n q x -> q n x"), in_=table_sb[:].rearrange("q n h x -> q (n h) x")
         )
-        blocked = out[LAST, HEADS - 3, 0:HALF, :]
-        for i in range(HALF // BLOCK):
-            nc.sync.dma_start(
-                out=blocked[BLOCK * i : BLOCK * (i + 1), :].rearrange("m (a x) -> a m x", x=CELL),
-                in_=table_sb[HALF + BLOCK * i : HALF + BLOCK * (i + 1), 1, :].rearrange("a (m x) -> a m x", x=CELL),
-            )
+        by_piece = piece_rows[0 : 32 * PIECES : 32]
+        first_batches = parked.rearrange("(n h) q x -> n (h q) x", h=2)[:, 0 : LAST * HALF, :]
+        nc.sync.dma_start(
+            out=by_piece[:, 0 : LAST_FROM // 2, :],
+            in_=first_batches.rearrange("n (u r) x -> n u r x", r=2 * ROWS)[:, :, 2 * ROWS - 1, :],
+        )
+        blocked = out[LAST, HEADS - 3 * PIECES : HEADS - 2 * PIECES, 0:HALF, :]
+        for piece in range(PIECES):
+            for i in range(HALF // BLOCK):
+                nc.sync.dma_start(
+                    out=blocked[piece, BLOCK * i : BLOCK * (i + 1), :].rearrange("m (a x) -> a m x", x=CELL),
+                    in_=table_sb[HALF + BLOCK * i : HALF + BLOCK * (i + 1), piece, 1, :].rearrange(
+                        "a (m x) -> a m x", x=CELL
+                    ),
+                )
         last_rows = setup.tile([P, POINTS], F32)
         nc.gpsimd.memset(last_rows[:], 0.0)
-        nc.sync.dma_start(out=last_rows[0:HALF, :], in_=blocked)
+        nc.sync.dma_start(out=last_rows[0:HALF, :], in_=blocked[0])
         for s in MADE:
             if s >= LAST_FROM:
                 i, m = LAST_STEPS[s - LAST_FROM][ROWS - 1]
-                row = BLOCK * i + m
-                nc.sync.dma_start(out=made_rows[0:1, s // 2, :], in_=blocked[row : row + 1, :])
+                nc.sync.dma_start(out=by_piece[:, s // 2, :], in_=blocked[:, BLOCK * i + m, :])
         last_dist = const.tile([P, HALF], F32)
 
         def run_of_pairs(s, r):
@@ -464,6 +475,9 @@ def tile_distancerelativebias_kernel(tc, coords, w1, b1, w2_words, w2_scales, b2
                 pairs[tick - 3] = regroup(tick - 3, *channels[tick - 3])
             if live(tick - 6):
                 vector_writes(tick - 6, sums[tick - 6], images[batch_of(tick - 6)])
+            if tick in ROUND_TICKS:
+                u = ROUND_TICKS[tick]
+                nc.vector.tensor_copy(out=made_rows[:, u.start : u.stop, :], in_=piece_rows[:, u.start : u.stop, :])
             if tick == LAST_DIST_TICK:
                 last_ps = psum_spread.tile([P, POINTS], F32, tag="spread")
                 nc.tensor.transpose(last_ps[:], last_rows[:], ident[:])

@@ -11,6 +11,7 @@ U8 = mybir.dt.uint8
 FP8X4 = mybir.dt.float8_e4m3fn_x4
 ACT = mybir.ActivationFunctionType
 ALU = mybir.AluOpType
+AXIS = mybir.AxisListType
 
 P = 128
 BATCH = 4
@@ -51,12 +52,17 @@ MADE = range(9, 64, 2)
 
 
 PIECES = 3
-ROUND_TICKS = {7: range(4, 8), 14: range(8, 14), 26: range(14, 20), 38: range(20, 26), 50: range(26, 32)}
+MADE_IN_BATCH = GROUPS // 2
+ROUND_TICKS = {7: slice(0, 1), 14: slice(1, BATCH)}
 LAST_DIST_TICK = 12
 
 
 def has_made_row(s):
     return s in MADE
+
+
+def made_index(s):
+    return s // GROUPS, s % GROUPS // 2
 
 
 def table_rows(s):
@@ -117,10 +123,9 @@ def tile_distancerelativebias_kernel(tc, coords, w1, b1, w2_words, w2_scales, b2
                 in_=w2_scales[0, 4 * quadrant : 4 * quadrant + 4, :].bitcast(I32),
             )
         rows_bf = setup.tile([P, HIDDEN], BF16)
-        nc.vector.memset(rows_bf[:], 0.0)
-        for piece in range(PIECES):
-            nc.sync.dma_start(out=rows_bf[32 * piece : 32 * piece + 1, :], in_=w1)
-        nc.sync.dma_start(out=rows_bf[96:97, :], in_=b1.rearrange("(o c) -> o c", o=1))
+        nc.sync.dma_start(out=rows_bf[0:64, :], in_=w1[0, :].partition_broadcast(64))
+        nc.sync.dma_start(out=rows_bf[64:96, :], in_=w1[0, :].partition_broadcast(32))
+        nc.sync.dma_start(out=rows_bf[96:128, :], in_=b1.partition_broadcast(32))
         b2_bf = setup.tile([P, 1], BF16)
         nc.sync.dma_start(out=b2_bf[:], in_=b2.rearrange("(k o) -> k o", o=1))
 
@@ -140,11 +145,20 @@ def tile_distancerelativebias_kernel(tc, coords, w1, b1, w2_words, w2_scales, b2
         ident = const.tile([P, P], F32)
         make_identity(nc, ident[:])
 
-        first_layer = const.tile([P, PACK, P], BF16)
-        made_rows = const.tile([P, STEPS // 2, POINTS], BF16)
-        piece_rows = setup.tile([P, STEPS // 2, POINTS], F32)
-        nc.gpsimd.memset(piece_rows[:, MADE[0] // 2 :, :], 0.0)
-        nc.gpsimd.memset(piece_rows[96:97, MADE[0] // 2 :, :], 1.0)
+        piece_rows = setup.tile([P, BATCH, POINTS], F32)
+        nc.gpsimd.memset(piece_rows[:], 0.0)
+        nc.gpsimd.memset(piece_rows[96:128, :, :], 1.0)
+        made_rows = const.tile([P, BATCH, POINTS], BF16)
+        pick = setup.tile([P, 32], F32)
+        nc.vector.tensor_reduce(
+            out=pick[:], in_=ident_bf[:].rearrange("x (k j) -> x j k", j=32), axis=AXIS.X, op=ALU.add
+        )
+        first_layer = const.tile([P, MADE_IN_BATCH, PACK, P], BF16)
+        for j in range(MADE_IN_BATCH):
+            nc.gpsimd.tensor_scalar(
+                out=first_layer[:, j], in0=rows_bf[:].rearrange("p (m t) -> p t m", t=PACK),
+                scalar1=pick[:, j : j + 1], scalar2=0.0, op0=ALU.mult, op1=ALU.add,
+            )
 
         diff = setup.tile([P, DIMS, BATCH, 2, HALF], F32)
         square = setup.tile([P, DIMS, BATCH, 2, HALF], F32)
@@ -181,7 +195,6 @@ def tile_distancerelativebias_kernel(tc, coords, w1, b1, w2_words, w2_scales, b2
 
         b2_col = const.tile([P, 1], F32)
         nc.vector.tensor_copy(out=b2_col[:], in_=b2_bf[:])
-        nc.vector.tensor_copy(out=first_layer[:], in_=rows_bf[:].rearrange("o (m t) -> o t m", t=PACK))
         table_ps = psum_spread.tile([P, 2, POINTS], F32, tag="spread")
         for h in range(2):
             nc.tensor.transpose(
@@ -198,12 +211,12 @@ def tile_distancerelativebias_kernel(tc, coords, w1, b1, w2_words, w2_scales, b2
         nc.sync.dma_start(
             out=parked.rearrange("n q x -> q n x"), in_=table_sb[:].rearrange("q n h x -> q (n h) x")
         )
-        by_piece = piece_rows[0 : 32 * PIECES : 32]
-        first_batches = parked.rearrange("(n h) q x -> n (h q) x", h=2)[:, 0 : LAST * HALF, :]
-        nc.sync.dma_start(
-            out=by_piece[:, 0 : LAST_FROM // 2, :],
-            in_=first_batches.rearrange("n (u r) x -> n u r x", r=2 * ROWS)[:, :, 2 * ROWS - 1, :],
-        )
+        first_batches = parked.rearrange("(k h) q x -> k (h q) x", h=2)[:, 0 : LAST * HALF, :]
+        for piece in range(PIECES):
+            nc.sync.dma_start(
+                out=piece_rows[32 * piece : 32 * piece + MADE_IN_BATCH, 0:LAST, :],
+                in_=first_batches[piece].rearrange("(n j r) x -> j n r x", n=LAST, r=2 * ROWS)[:, :, 2 * ROWS - 1, :],
+            )
         blocked = out[LAST, HEADS - 3 * PIECES : HEADS - 2 * PIECES, 0:HALF, :]
         for piece in range(PIECES):
             for i in range(HALF // BLOCK):
@@ -219,7 +232,8 @@ def tile_distancerelativebias_kernel(tc, coords, w1, b1, w2_words, w2_scales, b2
         for s in MADE:
             if s >= LAST_FROM:
                 i, m = LAST_STEPS[s - LAST_FROM][ROWS - 1]
-                nc.sync.dma_start(out=by_piece[:, s // 2, :], in_=blocked[:, BLOCK * i + m, :])
+                n, j = made_index(s)
+                nc.sync.dma_start(out=piece_rows[j : 32 * PIECES : 32, n, :], in_=blocked[:, BLOCK * i + m, :])
         last_dist = const.tile([P, HALF], F32)
 
         def run_of_pairs(s, r):
@@ -237,9 +251,10 @@ def tile_distancerelativebias_kernel(tc, coords, w1, b1, w2_words, w2_scales, b2
             if not has_made_row(s):
                 return spread, None
             made = psum_spread.tile([P, PACK, POINTS], F32, tag="spread")
+            n, j = made_index(s)
             for t in range(PACK):
                 nc.tensor.matmul(
-                    out=made[:, t, :], lhsT=first_layer[:, t, :], rhs=made_rows[:, s // 2, :], start=True, stop=True
+                    out=made[:, t, :], lhsT=first_layer[:, j, t, :], rhs=made_rows[:, n, :], start=True, stop=True
                 )
             return spread, made
 
@@ -476,8 +491,7 @@ def tile_distancerelativebias_kernel(tc, coords, w1, b1, w2_words, w2_scales, b2
             if live(tick - 6):
                 vector_writes(tick - 6, sums[tick - 6], images[batch_of(tick - 6)])
             if tick in ROUND_TICKS:
-                u = ROUND_TICKS[tick]
-                nc.vector.tensor_copy(out=made_rows[:, u.start : u.stop, :], in_=piece_rows[:, u.start : u.stop, :])
+                nc.vector.tensor_copy(out=made_rows[:, ROUND_TICKS[tick]], in_=piece_rows[:, ROUND_TICKS[tick]])
             if tick == LAST_DIST_TICK:
                 last_ps = psum_spread.tile([P, POINTS], F32, tag="spread")
                 nc.tensor.transpose(last_ps[:], last_rows[:], ident[:])

from contextlib import ExitStack

import concourse.mybir as mybir
from concourse.masks import make_identity

F32 = mybir.dt.float32
BF16 = mybir.dt.bfloat16
I32 = mybir.dt.int32
U32 = mybir.dt.uint32
U8 = mybir.dt.uint8
FP8X4 = mybir.dt.float8_e4m3fn_x4
ACT = mybir.ActivationFunctionType
ALU = mybir.AluOpType
AXIS = mybir.AxisListType

P = 128
BATCH = 4
POINTS = 128
HALF = POINTS // 2
DIMS = 3
HIDDEN = 512
HEADS = 128
PACK = 4
ROWS = 4
STEP_PAIRS = ROWS * POINTS
GROUPS = HALF // ROWS
STORE_ROWS = 16
MIRROR_GROUPS = GROUPS // 2
POINT_PITCH = 16
LAST = BATCH - 1
LAST_FROM = LAST * GROUPS
BLOCK = 16
CELL = 8
FOLDS = [(i, 2 * i + h) for i in range(4) for h in range(2)]
STRIPS = (
    [(i, m) for i in range(4) for m in range(2 * i + 2, 16)]
    + [(i, 2 * j + h) for j in range(3) for i in range(j + 1, 4) for h in range(2)]
)
FOLD_STEPS = len(FOLDS) // 2
IN_ORDER = STRIPS[2 * FOLD_STEPS :]
LAST_STEPS = (
    [FOLDS[2 * n : 2 * n + 2] + STRIPS[2 * n : 2 * n + 2] for n in range(FOLD_STEPS)]
    + [IN_ORDER[n : n + ROWS] for n in range(0, len(IN_ORDER) - 2 * ROWS, ROWS)]
    + [IN_ORDER[-8:-6], IN_ORDER[-6:-2], IN_ORDER[-2:]]
)
STRIPS_FROM = LAST_FROM + FOLD_STEPS
STEPS = LAST_FROM + len(LAST_STEPS)
COMPLETE = {53: [0], 56: [1], 58: [2], 60: [3], 62: [4], 63: [5], 64: [6, 7]}
SCALAR_COLS = 24
SCALAR_ALONE_FROM = STEPS - 5
MADE = range(9, 64, 2)


PIECES = 3
MADE_IN_BATCH = GROUPS // 2
ROUND_TICKS = {7: slice(0, 1), 14: slice(1, BATCH)}
LAST_DIST_TICK = 12


def has_made_row(s):
    return s in MADE


def made_index(s):
    return s // GROUPS, s % GROUPS // 2


def table_rows(s):
    return ROWS if s < LAST_FROM else len(LAST_STEPS[s - LAST_FROM])


def segments(cells):
    runs = []
    for n, (i, m) in enumerate(cells):
        if runs and runs[-1][1] == i and runs[-1][2] + runs[-1][3] == m:
            runs[-1] = runs[-1][:3] + (runs[-1][3] + 1,)
        else:
            runs.append((n, i, m, 1))
    return runs


IMAGE = POINTS * POINTS + POINTS

FLOPS = 2 * BATCH * POINTS * POINTS * HIDDEN * HEADS


def tile_distancerelativebias_kernel(tc, coords, w1, b1, w2_words, w2_scales, b2, out):
    nc = tc.nc
    with ExitStack() as ctx:
        const = ctx.enter_context(tc.tile_pool(name="const", bufs=1))
        setup = ctx.enter_context(tc.tile_pool(name="setup", bufs=1))
        hidden_pool = ctx.enter_context(tc.tile_pool(name="hidden", bufs=4))
        pair_pool = ctx.enter_context(tc.tile_pool(name="pair", bufs=3))
        mx_pool = ctx.enter_context(tc.tile_pool(name="mx", bufs=3))
        image_pool = ctx.enter_context(tc.tile_pool(name="image", bufs=2))
        psum_spread = ctx.enter_context(tc.psum_pool(name="psum_spread", bufs=5))
        psum_acc = ctx.enter_context(tc.psum_pool(name="psum_acc", bufs=3))
        ctx.enter_context(tc.manual_schedule())

        warm = setup.tile([P, 1], F32)
        nc.vector.memset(warm[:], 1.0)
        nc.scalar.activation(out=warm[:], in_=warm[:], func=ACT.Sqrt)

        by_point = coords.rearrange("b x c -> x b c")
        points = setup.tile([P, 2, POINT_PITCH], BF16)
        by_batch = points[:, :, 0 : BATCH * DIMS].rearrange("x h (b c) -> x b h c", c=DIMS)
        nc.sync.dma_start(out=by_batch[:, :, 0, :], in_=by_point)
        nc.sync.dma_start(out=by_batch[0:HALF, :, 1, :], in_=by_point[HALF:POINTS])
        nc.sync.dma_start(out=by_batch[HALF:POINTS, :, 1, :], in_=by_point[0:HALF])
        w1_bf = setup.tile([P, PACK], BF16)
        nc.sync.dma_start(out=w1_bf[:], in_=w1.rearrange("o (p t) -> (o p) t", t=PACK))
        b1_bf = setup.tile([P, PACK], BF16)
        nc.sync.dma_start(out=b1_bf[:], in_=b1.rearrange("(p t) -> p t", t=PACK))
        w2_codes = const.tile([P, HEADS], U32, align_bytes=64)
        nc.sync.dma_start(
            out=w2_codes[:].bitcast(I32), in_=w2_words[0].rearrange("p k t -> p (k t)").bitcast(I32)
        )
        w2_plane = const.tile([P, HEADS], U8, align_bytes=64)
        nc.vector.memset(w2_plane[:].bitcast(I32), 0)
        for quadrant in range(4):
            nc.sync.dma_start(
                out=w2_plane[32 * quadrant : 32 * quadrant + 4, :].bitcast(I32),
                in_=w2_scales[0, 4 * quadrant : 4 * quadrant + 4, :].bitcast(I32),
            )
        rows_bf = setup.tile([P, HIDDEN], BF16)
        nc.sync.dma_start(out=rows_bf[0:64, :], in_=w1[0, :].partition_broadcast(64))
        nc.sync.dma_start(out=rows_bf[64:96, :], in_=w1[0, :].partition_broadcast(32))
        nc.sync.dma_start(out=rows_bf[96:128, :], in_=b1.partition_broadcast(32))
        b2_bf = setup.tile([P, 1], BF16)
        nc.sync.dma_start(out=b2_bf[:], in_=b2.rearrange("(k o) -> k o", o=1))

        ident_bf = setup.tile([P, P], BF16)
        make_identity(nc, ident_bf[:])
        keep = const.tile([P, 2, HALF], F32)
        nc.gpsimd.memset(keep[:], 1.0)
        nc.gpsimd.affine_select(
            out=keep[:, 0, :], in_=keep[:, 0, :], pattern=[[-1, HALF]], base=0, channel_multiplier=1,
            compare_op=ALU.is_ge, fill=0.0,
        )
        nc.gpsimd.affine_select(
            out=keep[:, 1, :], in_=keep[:, 1, :], pattern=[[1, HALF]], base=-1, channel_multiplier=-1,
            compare_op=ALU.is_ge, fill=0.0,
        )

        ident = const.tile([P, P], F32)
        make_identity(nc, ident[:])

        piece_rows = setup.tile([P, BATCH, POINTS], F32)
        nc.gpsimd.memset(piece_rows[:], 0.0)
        nc.gpsimd.memset(piece_rows[96:128, :, :], 1.0)
        made_rows = const.tile([P, BATCH, POINTS], BF16)
        pick = setup.tile([P, 32], F32)
        nc.vector.tensor_reduce(
            out=pick[:], in_=ident_bf[:].rearrange("x (k j) -> x j k", j=32), axis=AXIS.X, op=ALU.add
        )
        first_layer = const.tile([P, MADE_IN_BATCH, PACK, P], BF16)
        for j in range(MADE_IN_BATCH):
            nc.gpsimd.tensor_scalar(
                out=first_layer[:, j], in0=rows_bf[:].rearrange("p (m t) -> p t m", t=PACK),
                scalar1=pick[:, j : j + 1], scalar2=0.0, op0=ALU.mult, op1=ALU.add,
            )

        diff = setup.tile([P, DIMS, BATCH, 2, HALF], F32)
        square = setup.tile([P, DIMS, BATCH, 2, HALF], F32)
        for c in range(DIMS):
            spread = psum_spread.tile([P, BATCH, POINTS], BF16, tag="spread")
            for b in range(BATCH):
                column = points[:, 0, DIMS * b + c : DIMS * b + c + 1]
                nc.tensor.transpose(spread[:, b, :], column.to_broadcast([P, P]), ident_bf[:])
            nc.vector.tensor_tensor(
                out=diff[:, c],
                in0=spread[:].rearrange("p b (h a) -> p b h a", h=2),
                in1=by_batch[:, :, :, c].unsqueeze(3).to_broadcast([P, BATCH, 2, HALF]),
                op=ALU.subtract,
            )
            nc.scalar.activation(out=square[:, c], in_=diff[:, c], func=ACT.Square)
        w1_col = const.tile([P, PACK], F32)
        nc.vector.tensor_copy(out=w1_col[:], in_=w1_bf[:])
        b1_col = const.tile([P, PACK], F32)
        nc.vector.tensor_copy(out=b1_col[:], in_=b1_bf[:])
        both = setup.tile([P, BATCH, 2, HALF], F32)
        dist_sq = setup.tile([P, BATCH, HALF], F32)
        dist = const.tile([P, BATCH, HALF], F32)
        halves = (slice(0, BATCH // 2), slice(BATCH // 2, BATCH))
        for h in halves:
            nc.vector.tensor_tensor(out=both[:, h], in0=square[:, 0, h], in1=square[:, 1, h], op=ALU.add)
        for h in halves:
            nc.vector.tensor_tensor(out=both[:, h], in0=both[:, h], in1=square[:, 2, h], op=ALU.add)
        keep_both = keep[:].unsqueeze(1).to_broadcast([P, BATCH // 2, 2, HALF])
        for h in halves:
            nc.vector.tensor_tensor(out=both[:, h], in0=both[:, h], in1=keep_both, op=ALU.mult)
        for h in halves:
            nc.vector.tensor_tensor(out=dist_sq[:, h], in0=both[:, h, 0, :], in1=both[:, h, 1, :], op=ALU.add)
            nc.scalar.activation(out=dist[:, h], in_=dist_sq[:, h], func=ACT.Sqrt)

        b2_col = const.tile([P, 1], F32)
        nc.vector.tensor_copy(out=b2_col[:], in_=b2_bf[:])
        table_ps = psum_spread.tile([P, 2, POINTS], F32, tag="spread")
        for h in range(2):
            nc.tensor.transpose(
                table_ps[:, h, :], dist[:, 2 * h : 2 * h + 2, :].rearrange("x b a -> x (b a)"), ident[:]
            )
        table_sb = setup.tile([P, PIECES, 2, POINTS], F32)
        rounded = setup.tile([P, PIECES - 1, 2, POINTS], BF16)
        nc.vector.tensor_copy(out=table_sb[:, 0], in_=table_ps[:])
        nc.vector.tensor_copy(out=rounded[:, 0], in_=table_ps[:])
        nc.vector.tensor_tensor(out=table_sb[:, 1], in0=table_sb[:, 0], in1=rounded[:, 0], op=ALU.subtract)
        nc.vector.tensor_copy(out=rounded[:, 1], in_=table_sb[:, 1])
        nc.vector.tensor_tensor(out=table_sb[:, 2], in0=table_sb[:, 1], in1=rounded[:, 1], op=ALU.subtract)
        parked = out[LAST, HEADS - 2 * PIECES : HEADS, :, :]
        nc.sync.dma_start(
            out=parked.rearrange("n q x -> q n x"), in_=table_sb[:].rearrange("q n h x -> q (n h) x")
        )
        first_batches = parked.rearrange("(k h) q x -> k (h q) x", h=2)[:, 0 : LAST * HALF, :]
        for piece in range(PIECES):
            nc.sync.dma_start(
                out=piece_rows[32 * piece : 32 * piece + MADE_IN_BATCH, 0:LAST, :],
                in_=first_batches[piece].rearrange("(n j r) x -> j n r x", n=LAST, r=2 * ROWS)[:, :, 2 * ROWS - 1, :],
            )
        blocked = out[LAST, HEADS - 3 * PIECES : HEADS - 2 * PIECES, 0:HALF, :]
        for piece in range(PIECES):
            for i in range(HALF // BLOCK):
                nc.sync.dma_start(
                    out=blocked[piece, BLOCK * i : BLOCK * (i + 1), :].rearrange("m (a x) -> a m x", x=CELL),
                    in_=table_sb[HALF + BLOCK * i : HALF + BLOCK * (i + 1), piece, 1, :].rearrange(
                        "a (m x) -> a m x", x=CELL
                    ),
                )
        last_rows = setup.tile([P, POINTS], F32)
        nc.gpsimd.memset(last_rows[:], 0.0)
        nc.sync.dma_start(out=last_rows[0:HALF, :], in_=blocked[0])
        for s in MADE:
            if s >= LAST_FROM:
                i, m = LAST_STEPS[s - LAST_FROM][ROWS - 1]
                n, j = made_index(s)
                nc.sync.dma_start(out=piece_rows[j : 32 * PIECES : 32, n, :], in_=blocked[:, BLOCK * i + m, :])
        last_dist = const.tile([P, HALF], F32)

        def run_of_pairs(s, r):
            if s < LAST_FROM:
                b, g = divmod(s, GROUPS)
                return dist[:, b, ROWS * g + r : ROWS * g + r + 1]
            i, m = LAST_STEPS[s - LAST_FROM][r]
            return last_dist[:, BLOCK * i + m : BLOCK * i + m + 1]

        def spread_distances(s):
            count = table_rows(s) - (1 if has_made_row(s) else 0)
            spread = psum_spread.tile([P, ROWS, POINTS], F32, tag="spread")
            for r in range(count):
                nc.tensor.transpose(spread[:, r, :], run_of_pairs(s, r).to_broadcast([P, P]), ident[:])
            if not has_made_row(s):
                return spread, None
            made = psum_spread.tile([P, PACK, POINTS], F32, tag="spread")
            n, j = made_index(s)
            for t in range(PACK):
                nc.tensor.matmul(
                    out=made[:, t, :], lhsT=first_layer[:, j, t, :], rhs=made_rows[:, n, :], start=True, stop=True
                )
            return spread, made

        def parts(s, count):
            return [(0, count // 2), (count // 2, count)] if s == 0 else [(0, count)]

        def hidden_layer(s, spread, made):
            count = POINTS * (table_rows(s) - (0 if made is None else 1))
            by_channel = hidden_pool.tile([P, PACK, STEP_PAIRS], BF16)
            by_pair = pair_pool.tile([P, STEP_PAIRS, PACK], BF16, align_bytes=64)
            for low, high in parts(s, count):
                for t in range(PACK):
                    nc.scalar.activation(
                        out=by_channel[:, t, low:high], in_=spread[:].rearrange("p r x -> p (r x)")[:, low:high],
                        func=ACT.Silu, scale=w1_col[:, t : t + 1], bias=b1_col[:, t : t + 1],
                    )
            if made is not None:
                nc.scalar.activation(
                    out=by_pair[:, count : count + POINTS, :], in_=made[:].rearrange("p t n -> p n t"), func=ACT.Silu
                )
            return by_channel, by_pair, count

        def regroup(s, by_channel, by_pair, count):
            for low, high in parts(s, count):
                nc.vector.tensor_copy(
                    out=by_pair[:, low:high, :].rearrange("p (n i) (u v) -> p n u i v", i=4, u=2),
                    in_=by_channel[:, :, low:high].rearrange("p (u v) (n i) -> p n u i v", i=4, u=2),
                )
            return by_pair

        def quantise(s, by_pair):
            count = POINTS * table_rows(s)
            codes = mx_pool.tile([P, STEP_PAIRS], U32, align_bytes=64)
            plane = mx_pool.tile([P, STEP_PAIRS], U8, align_bytes=64)
            nc.vector.quantize_mx(
                out=codes[:, 0:count].bitcast(FP8X4), scales=plane[:, 0:count],
                in_=by_pair[:, 0:count, :].rearrange("p n t -> p (n t)"),
            )
            return codes, plane, count

        def multiply(codes, plane, count):
            acc = psum_acc.tile([P, STEP_PAIRS], F32)
            nc.tensor.matmul_mx(
                out=acc[:, 0:count],
                lhsT=w2_codes[:].bitcast(FP8X4), lhsT_scale=w2_plane[:],
                rhs=codes[:, 0:count].bitcast(FP8X4), rhs_scale=plane[:, 0:count],
                start=True, stop=True,
            )
            return acc[:, 0:count]

        def image_rows(image):
            return image[:, 0 : POINTS * POINTS].rearrange("k (i j) -> k i j", j=POINTS)

        def vector_write(dst, src):
            nc.vector.tensor_scalar_add(out=dst, in0=src, scalar1=b2_col[:, 0:1])

        def scalar_write(dst, src):
            nc.scalar.activation(out=dst, in_=src, func=ACT.Identity, bias=b2_col[:, 0:1], scale=1.0)

        def mirror(dst, src):
            nc.gpsimd.tensor_scalar(
                out=dst.rearrange("k x (n r) -> k n x r", r=4), in0=src.rearrange("k (n r) x -> k n x r", r=4),
                scalar1=1.0, scalar2=0.0, op0=ALU.mult, op1=ALU.add,
            )


        def table_scalar_writes(g, acc, rows):
            a0 = ROWS * g
            by_row = acc.rearrange("k (r x) -> k r x", x=POINTS)
            first = POINTS - SCALAR_COLS
            scalar_write(rows[:, a0 : a0 + ROWS, first:POINTS], by_row[:, :, first:POINTS])

        def table_vector_writes(g, acc, rows):
            a0 = ROWS * g
            a1 = a0 + ROWS
            by_row = acc.rearrange("k (r x) -> k r x", x=POINTS)
            by_x = acc.rearrange("k (r x) -> k x r", x=POINTS)
            vector_write(rows[:, HALF : HALF + a1, HALF + a0 : HALF + a1], by_x[:, 0:a1, :])
            if a0 > 0:
                vector_write(rows[:, HALF + a0 : HALF + a1, HALF : HALF + a0], by_row[:, :, 0:a0])
            if a1 < HALF:
                vector_write(rows[:, a1:HALF, a0:a1], by_x[:, a1:HALF, :])
            first = POINTS - SCALAR_COLS
            vector_write(rows[:, a0:a1, a0:first], by_row[:, :, a0:first])
            mirror(rows[:, HALF:POINTS, a0:a1], rows[:, a0:a1, HALF:POINTS])

        def place(i, m):
            if m < 2 * i:
                return HALF + BLOCK * i, HALF + CELL * m
            return BLOCK * i, CELL * m

        def first_places(write, acc, rows, cells):
            for n, i, m, count in segments([cell[1:] for cell in cells]):
                a0, x0 = place(i, m)
                c = cells[n][0]
                write(
                    rows[:, a0 : a0 + BLOCK, x0 : x0 + CELL * count].rearrange("k a (c x) -> k c a x", x=CELL),
                    acc[:, POINTS * c : POINTS * (c + count)].rearrange("k (c a x) -> k c a x", a=BLOCK, x=CELL),
                )

        def second_places(write, acc, rows, cells):
            for n, i, m, count in segments([cell[1:] for cell in cells]):
                a0, x0 = place(i, m)
                c = cells[n][0]
                write(
                    rows[:, x0 : x0 + CELL * count, a0 : a0 + BLOCK].rearrange("k (c x) a -> k c x a", x=CELL),
                    acc[:, POINTS * c : POINTS * (c + count)].rearrange("k (c a x) -> k c x a", a=BLOCK, x=CELL),
                )

        def strip_shares(s):
            cells = [(c,) + cell for c, cell in enumerate(LAST_STEPS[s - LAST_FROM])]
            if s >= STEPS - 2:
                return cells, [], [], cells, []
            if s >= SCALAR_ALONE_FROM:
                half = 2 if len(cells) == ROWS else 0
                return cells, cells[half:], [], [], cells[:half]
            by_scalar = cells[3:]
            by_vector = [cell for cell in cells if cell not in by_scalar]
            if s < STRIPS_FROM:
                return by_scalar, [], by_vector[2:], [], cells[2:]
            return by_scalar, [], by_vector, cells[2:], cells[:2]

        def strip_scalar_writes(s, acc, rows):
            first, second = strip_shares(s)[:2]
            first_places(scalar_write, acc, rows, first)
            second_places(scalar_write, acc, rows, second)

        def strip_vector_writes(s, acc, rows):
            first, second, mirrored = strip_shares(s)[2:]
            second_places(vector_write, acc, rows, second)
            first_places(vector_write, acc, rows, first)
            for n, i, m, count in segments([cell[1:] for cell in mirrored]):
                a0, x0 = place(i, m)
                mirror(
                    rows[:, x0 : x0 + CELL * count, a0 : a0 + BLOCK], rows[:, a0 : a0 + BLOCK, x0 : x0 + CELL * count]
                )

        def fold_vector_writes(s, acc, rows):
            i = LAST_STEPS[s - LAST_FROM][0][0]
            low, high = BLOCK * i, HALF + BLOCK * i
            fold = acc[:, 0 : 2 * POINTS]
            vector_write(
                rows[:, low : low + BLOCK, low : low + BLOCK].rearrange("k a (c x) -> k c a x", x=CELL),
                fold.rearrange("k (c a x) -> k c a x", a=BLOCK, x=CELL),
            )
            vector_write(
                rows[:, high : high + BLOCK, high : high + BLOCK].rearrange("k (c x) a -> k c x a", x=CELL),
                fold.rearrange("k (c a x) -> k c x a", a=BLOCK, x=CELL),
            )

        def mirror_quarters(image):
            pitch = BLOCK * POINTS + BLOCK
            blocks = image[:, 0 : POINTS // BLOCK * pitch].rearrange("k (q e) -> k q e", e=pitch)
            by_row = blocks[:, :, 0 : BLOCK * POINTS].rearrange("k q (i j) -> k q i j", j=POINTS)
            nc.gpsimd.tensor_scalar(
                out=by_row[:, :, CELL:BLOCK, 0:CELL],
                in0=by_row[:, :, 0:CELL, CELL:BLOCK].rearrange("k q r x -> k q x r"),
                scalar1=1.0, scalar2=0.0, op0=ALU.mult, op1=ALU.add,
            )

        def mirror_blocks(image, size, first, last):
            pitch = size * POINTS + size
            blocks = image[:].rearrange("k (h q e) -> k h q e", h=2, e=pitch)[:, :, first:last, :]
            for r in range(1, size):
                nc.gpsimd.tensor_scalar(
                    out=blocks[:, :, :, POINTS * r : POINTS * r + r],
                    in0=blocks[:, :, :, r : r + POINTS * (r - 1) + 1 : POINTS],
                    scalar1=1.0, scalar2=0.0, op0=ALU.mult, op1=ALU.add,
                )

        def store(b, image, first_row, count):
            nc.sync.dma_start(
                out=out[b, :, first_row : first_row + count, :],
                in_=image_rows(image)[:, first_row : first_row + count, :],
            )

        def scalar_writes(s, acc, image):
            rows = image_rows(image)
            if s < LAST_FROM:
                table_scalar_writes(s % GROUPS, acc, rows)
            else:
                strip_scalar_writes(s, acc, rows)

        def vector_writes(s, acc, image):
            rows = image_rows(image)
            if s < LAST_FROM:
                b, g = divmod(s, GROUPS)
                table_vector_writes(g, acc, rows)
                if g % MIRROR_GROUPS == MIRROR_GROUPS - 1:
                    mirror_blocks(image, ROWS, g + 1 - MIRROR_GROUPS, g + 1)
                    for first_row in range(ROWS * (g + 1 - MIRROR_GROUPS), ROWS * (g + 1), STORE_ROWS):
                        store(b, image, first_row, STORE_ROWS)
                if g == GROUPS - 1:
                    for first_row in range(HALF, POINTS, STORE_ROWS):
                        store(b, image, first_row, STORE_ROWS)
            else:
                if s < STRIPS_FROM:
                    fold_vector_writes(s, acc, rows)
                strip_vector_writes(s, acc, rows)
                if s == STRIPS_FROM - 1:
                    mirror_quarters(image)
                if s == STRIPS_FROM:
                    mirror_blocks(image, CELL, 0, HALF // CELL)
                for n in COMPLETE.get(s, []):
                    store(LAST, image, STORE_ROWS * n, STORE_ROWS)

        spreads, channels, pairs, quantised, sums, images = {}, {}, {}, {}, {}, {}

        def live(s):
            return 0 <= s < STEPS

        def batch_of(s):
            return min(s // GROUPS, LAST)

        for tick in range(STEPS + 7):
            if live(tick):
                spreads[tick] = spread_distances(tick)
            if live(tick - 2):
                channels[tick - 2] = hidden_layer(tick - 2, *spreads[tick - 2])
            if tick == LAST_DIST_TICK + 1:
                nc.scalar.copy(out=last_dist[:], in_=last_ps[:, 0:HALF])
            if tick - 5 in range(0, STEPS, GROUPS) and tick - 5 <= LAST_FROM:
                image = image_pool.tile([P, IMAGE], F32)
                images[batch_of(tick - 5)] = image
            if tick == STEPS + 1:
                scalar_writes(SCALAR_ALONE_FROM, sums[SCALAR_ALONE_FROM], images[LAST])
            if live(tick - 5) and tick - 5 != SCALAR_ALONE_FROM:
                scalar_writes(tick - 5, sums[tick - 5], images[batch_of(tick - 5)])
            if live(tick - 4):
                quantised[tick - 4] = quantise(tick - 4, pairs[tick - 4])
                sums[tick - 4] = multiply(*quantised[tick - 4])
            if live(tick - 3):
                pairs[tick - 3] = regroup(tick - 3, *channels[tick - 3])
            if live(tick - 6):
                vector_writes(tick - 6, sums[tick - 6], images[batch_of(tick - 6)])
            if tick in ROUND_TICKS:
                nc.vector.tensor_copy(out=made_rows[:, ROUND_TICKS[tick]], in_=piece_rows[:, ROUND_TICKS[tick]])
            if tick == LAST_DIST_TICK:
                last_ps = psum_spread.tile([P, POINTS], F32, tag="spread")
                nc.tensor.transpose(last_ps[:], last_rows[:], ident[:])
